import numpy as np
import ml_dtypes


def mxq(x, axis, fmt="e4m3"):
    dtype, down = {"e4m3": (ml_dtypes.float8_e4m3fn, 7), "e5m2": (ml_dtypes.float8_e5m2, 14)}[fmt]
    v = np.moveaxis(np.asarray(x, np.float32).astype(ml_dtypes.bfloat16).astype(np.float64), axis, -1)
    blocks = v.reshape(v.shape[:-1] + (-1, 32))
    amax = np.abs(blocks).max(-1, keepdims=True)
    byte = np.maximum(np.where(amax > 0, np.frexp(amax)[1] - 1 + 127, 0) - down, 1)
    scale = np.exp2(byte - 127.0)
    codes = (blocks / scale).astype(np.float32).astype(dtype).astype(np.float64)
    return np.moveaxis((codes * scale).reshape(v.shape), -1, axis)


WIDE = False


def mx_kscale(k):
    if not WIDE:
        return np.ones(k)
    levels = np.array([10, -10, 5, -5, 0])
    a = np.random.permutation(np.resize(levels, k // 512 * 4)).reshape(k // 512, 4)
    idx = np.arange(k)
    return np.exp2(a[idx // 512, idx % 128 // 32])


BF16 = ml_dtypes.bfloat16


def bf(x):
    return np.asarray(x, np.float32).astype(BF16)


def f64(x):
    return np.asarray(x).astype(np.float64)


E2M1 = np.array([0.0, 0.5, 1.0, 1.5, 2.0, 3.0, 4.0, 6.0, -0.0, -0.5, -1.0, -1.5, -2.0, -3.0, -4.0, -6.0])


def pack_weight(w, fmt):
    k, n = w.shape
    w = f64(bf(w)).reshape(k // 32, 32, n)
    amax = np.abs(w).max(1)
    if fmt == "e4m3":
        byte = np.frexp(amax)[1] - 1 + 127 - 7
    else:
        mant, ex = np.frexp(amax / 6.0)
        byte = np.where(mant > 0.5, ex, ex - 1) + 127
    byte = np.clip(np.where(amax > 0, byte, 1), 1, 254)
    scaled = (w * np.exp2(127.0 - byte)[:, None, :]).reshape(k, n).astype(np.float32)
    by_word = np.ascontiguousarray(scaled.reshape(k // 512, 128, 4, n).transpose(0, 1, 3, 2))
    if fmt == "e4m3":
        words = by_word.astype(ml_dtypes.float8_e4m3fn).view(np.uint8)
    else:
        c = by_word.astype(ml_dtypes.float4_e2m1fn).view(np.uint8) & 0xF
        words = c[..., 0::2] | (c[..., 1::2] << 4)
    return np.ascontiguousarray(words), np.ascontiguousarray(byte.astype(np.uint8).reshape(k // 512, 16, n))


def unpack_weight(words, scales, fmt):
    g, p, n, _ = words.shape
    if fmt == "e4m3":
        vals = np.ascontiguousarray(words).view(ml_dtypes.float8_e4m3fn).astype(np.float64)
    else:
        nib = np.empty((g, p, n, 4), np.uint8)
        nib[..., 0::2] = words & 0xF
        nib[..., 1::2] = words >> 4
        vals = E2M1[nib]
    vals = vals * np.repeat(np.exp2(scales.astype(np.float64) - 127.0), 8, axis=1)[..., None]
    return vals.transpose(0, 1, 3, 2).reshape(g * 512, n)


H, S, QP, VP = 4, 512, 512, 512
HV = H * VP


def setup_inputs():
    s = mx_kscale(QP)
    q = bf(np.random.standard_normal((H, S, QP)) * 1.5)
    k = bf(np.random.standard_normal((H, S, QP)) * 1.5)
    value = bf(np.random.standard_normal((S, QP)) * s[None, :])
    mask = bf(np.random.random((S, S)))
    Wv = np.random.standard_normal((H, VP, QP)) * 1.5 / np.sqrt(QP) / s[None, None, :]
    Wv_words, Wv_scales = pack_weight(Wv.swapaxes(1, 2).reshape(-1, VP), "e4m3")
    bv = bf(np.random.standard_normal((H, VP)) * 0.3)
    return {
        "q": q,
        "k": k,
        "value": value,
        "mask": mask,
        "Wv_words": Wv_words,
        "Wv_scales": Wv_scales,
        "bv": bv,
    }


def reference(q, k, value, mask, Wv_words, Wv_scales, bv):
    v = (mxq(f64(value), 1, "e4m3") @ unpack_weight(Wv_words, Wv_scales, "e4m3").reshape(H, QP, VP)) + f64(bv)[:, None, :]
    s = (f64(q) @ f64(k).transpose(0, 2, 1)) * f64(mask)[None, :, :] * (1.0 / np.sqrt(QP))
    e = np.exp(s - s.max(-1, keepdims=True))
    o = (mxq(e, 2, "e4m3") @ mxq(v, 1, "e4m3")) / e.sum(-1, keepdims=True)
    return o.transpose(1, 0, 2).reshape(S, HV)

@@ -1,0 +1,235 @@
+from contextlib import ExitStack
+import math
+
+import concourse.mybir as mybir
+from concourse.masks import make_identity
+
+F32 = mybir.dt.float32
+BF16 = mybir.dt.bfloat16
+I32 = mybir.dt.int32
+U32 = mybir.dt.uint32
+U8 = mybir.dt.uint8
+FP8X4 = mybir.dt.float8_e4m3fn_x4
+ALU = mybir.AluOpType
+ACT = mybir.ActivationFunctionType
+AXIS = mybir.AxisListType
+
+P = 128
+PACK = 4
+HEADS = 4
+SEQ = 512
+DIM = 512
+TILES = SEQ // P
+STEPS = HEADS * TILES
+SCALE = 1.0 / math.sqrt(DIM)
+
+FLOPS = 3 * HEADS * 2 * SEQ * DIM * DIM
+
+
+def tile_maskedmultiheadattention_pa_e_kernel(tc, q, k, value, mask, Wv_words, Wv_scales, bv, out):
+    nc = tc.nc
+    with ExitStack() as ctx:
+        ctx.enter_context(tc.manual_schedule())
+        keep = ctx.enter_context(tc.tile_pool(name="keep", bufs=1))
+        flipped = ctx.enter_context(tc.tile_pool(name="flipped", bufs=2))
+        work = ctx.enter_context(tc.tile_pool(name="work", bufs=3))
+        score_banks = ctx.enter_context(tc.psum_pool(name="score_banks", bufs=3))
+        flip_banks = ctx.enter_context(tc.psum_pool(name="flip_banks", bufs=2))
+        mx_banks = ctx.enter_context(tc.psum_pool(name="mx_banks", bufs=3))
+
+        ident = keep.tile([P, P], F32, name="ident")
+        ones = keep.tile([P, P], BF16, name="ones")
+        bias_row = keep.tile([P, HEADS * DIM], BF16, name="bias_row")
+        bias_all = keep.tile([P, HEADS, DIM], F32, name="bias_all")
+        mask_sb = keep.tile([P, TILES, SEQ], BF16, name="mask_sb")
+        val_sb = keep.tile([P, PACK, DIM], BF16, name="val_sb")
+        val_grouped = keep.tile([P, PACK, P, PACK], BF16, name="val_grouped", align_bytes=64)
+        val_codes = keep.tile([P, SEQ], U32, name="val_codes", align_bytes=64)
+        val_scales = keep.tile([P, SEQ], U8, name="val_scales", align_bytes=64)
+        wv_codes = keep.tile([P, HEADS, DIM], U32, name="wv_codes", align_bytes=64)
+        wv_scales = keep.tile([P, HEADS, DIM], U8, name="wv_scales", align_bytes=64)
+        v_grouped = keep.tile([P, HEADS, DIM, PACK], BF16, name="v_grouped", align_bytes=64)
+        v_codes = keep.tile([P, HEADS, DIM], U32, name="v_codes", align_bytes=64)
+        v_scales = keep.tile([P, HEADS, DIM], U8, name="v_scales", align_bytes=64)
+        q_sb = [keep.tile([P, TILES, DIM], BF16, name="q_sb%d" % h) for h in range(HEADS)]
+        k_sb = [keep.tile([P, TILES, DIM], BF16, name="k_sb%d" % h) for h in range(HEADS)]
+        neg_max = keep.tile([P, STEPS], F32, name="neg_max")
+        row_sum = keep.tile([P, STEPS], F32, name="row_sum")
+        inv_sum = keep.tile([P, STEPS], F32, name="inv_sum")
+
+        nc.vector.memset(wv_scales[:].rearrange("p h n -> p (h n)").bitcast(I32), 0)
+        nc.vector.memset(bias_row[:].bitcast(I32), 0)
+        nc.vector.memset(ones[:], 1.0)
+        make_identity(nc, ident[:])
+
+        nc.scalar.dma_start(out=bias_row[0:1, :], in_=bv.rearrange("(o h) n -> o (h n)", o=1))
+        nc.sync.dma_start(out=val_sb[:], in_=value.rearrange("(p t) f -> p t f", t=PACK))
+        scale_words = Wv_scales.bitcast(I32)
+        for quad in range(4):
+            nc.sync.dma_start(
+                out=wv_scales[32 * quad : 32 * quad + 4, :, :].bitcast(I32),
+                in_=scale_words[:, 4 * quad : 4 * quad + 4, :].rearrange("h r n -> r h n"),
+            )
+        code_words = Wv_words.rearrange("h p n t -> h p (n t)").bitcast(I32)
+        nc.sync.dma_start(out=wv_codes[:, 0, :].bitcast(I32), in_=code_words[0])
+        nc.sync.dma_start(out=k_sb[0][:], in_=k[0].rearrange("(a p) d -> p a d", p=P))
+        nc.sync.dma_start(out=q_sb[0][:], in_=q[0].rearrange("(p a) d -> p a d", a=TILES))
+        nc.sync.dma_start(out=mask_sb[:], in_=mask.rearrange("(p a) j -> p a j", a=TILES))
+        nc.sync.dma_start(out=wv_codes[:, 1:HEADS, :].bitcast(I32), in_=code_words[1:HEADS].rearrange("h p w -> p h w"))
+        for h in range(1, HEADS):
+            nc.sync.dma_start(out=k_sb[h][:], in_=k[h].rearrange("(a p) d -> p a d", p=P))
+            nc.sync.dma_start(out=q_sb[h][:], in_=q[h].rearrange("(p a) d -> p a d", a=TILES))
+        out_rows = out.rearrange("(p a) n -> p a n", a=TILES)
+
+        def spread_bias(h):
+            spread = mx_banks.tile([P, DIM], F32, name="spread", tag="mx")
+            nc.tensor.matmul(out=spread[:], lhsT=ones[:], rhs=bias_row[:, h * DIM : (h + 1) * DIM], start=True, stop=True)
+            nc.scalar.copy(out=bias_all[:, h, :], in_=spread[:])
+
+        def quantise_value():
+            pairs = val_grouped[:].rearrange("f t j x -> f (t j x)").bitcast(F32).rearrange("f (t j u) -> f t j u", t=PACK, u=2)
+            for half in range(2):
+                bank = flip_banks.tile([P, 2, 2, P], F32, name="val_bank", tag="flip")
+                for tt in range(2):
+                    words = val_sb[:, 2 * half + tt, :].bitcast(F32)
+                    for u in range(2):
+                        nc.tensor.transpose(bank[:, tt, u, :], words[:, u : DIM // 2 : 2], ident[:])
+                nc.vector.tensor_copy(out=pairs[:, 2 * half : 2 * half + 2, :, :], in_=bank[:].rearrange("f tt u j -> f tt j u"))
+            nc.vector.quantize_mx(
+                out=val_codes[:].bitcast(FP8X4),
+                scales=val_scales[:],
+                in_=val_grouped[:].rearrange("f t j x -> f (t j x)"),
+            )
+
+        def project_values(h, part):
+            cols = slice(part * P, (part + 1) * P)
+            bank = mx_banks.tile([P, PACK, P], F32, name="v_bank", tag="mx")
+            for t in range(PACK):
+                nc.tensor.matmul_mx(
+                    out=bank[:, t, :],
+                    lhsT=val_codes[:, t * P : (t + 1) * P].bitcast(FP8X4),
+                    lhsT_scale=val_scales[:, t * P : (t + 1) * P],
+                    rhs=wv_codes[:, h, cols].bitcast(FP8X4),
+                    rhs_scale=wv_scales[:, h, cols],
+                    start=True,
+                    stop=True,
+                )
+            nc.vector.tensor_tensor(
+                out=v_grouped[:, h, cols, :],
+                in0=bank[:].rearrange("j t n -> j n t"),
+                in1=bias_all[:, h, cols].unsqueeze(2).to_broadcast([P, P, PACK]),
+                op=ALU.add,
+            )
+
+        def quantise_values(h, part):
+            cols = slice(part * P, (part + 1) * P)
+            nc.vector.quantize_mx(
+                out=v_codes[:, h, cols].bitcast(FP8X4),
+                scales=v_scales[:, h, cols],
+                in_=v_grouped[:, h, cols, :].rearrange("j n t -> j (n t)"),
+            )
+
+        def flip_features(rows_sb, cols_sb, chunk):
+            bank = flip_banks.tile([P, SEQ], F32, name="flip_bank", tag="flip")
+            for a in range(TILES):
+                nc.tensor.transpose(bank[:, a * P : (a + 1) * P], rows_sb[:, a, :].bitcast(F32)[:, chunk * P : (chunk + 1) * P], ident[:])
+            nc.scalar.copy(out=cols_sb[:, chunk, :, :].rearrange("w r e -> w (r e)"), in_=bank[:].bitcast(BF16))
+
+        def scores(n, qT, kT):
+            a = n % TILES
+            bank = score_banks.tile([P, SEQ], F32, name="s_bank", tag="s")
+            for i in range(4):
+                chunk, e = divmod(i, 2)
+                nc.tensor.matmul(out=bank[:], lhsT=qT[:, chunk, a * P : (a + 1) * P, e], rhs=kT[:, chunk, :, e], start=(i == 0), stop=(i == 3))
+            masked = work.tile([P, SEQ], F32, name="masked")
+            nc.vector.scalar_tensor_tensor(out=masked[:], in0=bank[:], scalar=SCALE, in1=mask_sb[:, a, :], op0=ALU.mult, op1=ALU.mult)
+            nc.vector.tensor_reduce(out=neg_max[:, n : n + 1], in_=masked[:], axis=AXIS.X, op=ALU.max, negate=True)
+            return masked
+
+        def exponentials(n, masked):
+            e_sb = work.tile([P, SEQ], BF16, name="e_sb")
+            nc.scalar.activation(out=e_sb[:], in_=masked[:], func=ACT.Exp, bias=neg_max[:, n : n + 1], scale=1.0, accum_out=row_sum[:, n : n + 1])
+            return e_sb
+
+        def flip_weights(e_sb):
+            bank = flip_banks.tile([P, 2, P], F32, name="e_bank", tag="flip")
+            words = e_sb[:].bitcast(F32)
+            for u in range(2):
+                nc.tensor.transpose(bank[:, u, :], words[:, u : SEQ // 2 : 2], ident[:])
+            e_grouped = work.tile([P, P, PACK], BF16, name="e_grouped", align_bytes=64)
+            pairs = e_grouped[:].rearrange("j i x -> j (i x)").bitcast(F32).rearrange("j (i u) -> j i u", u=2)
+            nc.scalar.copy(out=pairs, in_=bank[:].rearrange("j u i -> j i u"))
+            return e_grouped
+
+        def quantise_weights(n, e_grouped):
+            e_codes = work.tile([P, P], U32, name="e_codes", align_bytes=64)
+            e_scales = work.tile([P, P], U8, name="e_scales", align_bytes=64)
+            nc.vector.quantize_mx(out=e_codes[:].bitcast(FP8X4), scales=e_scales[:], in_=e_grouped[:].rearrange("j i x -> j (i x)"))
+            nc.vector.reciprocal(out=inv_sum[:, n : n + 1], in_=row_sum[:, n : n + 1])
+            return e_codes, e_scales
+
+        def weighted_values(n, e_codes, e_scales):
+            h, a = divmod(n, TILES)
+            bank = mx_banks.tile([P, DIM], F32, name="o_bank", tag="mx")
+            nc.tensor.matmul_mx(
+                out=bank[:],
+                lhsT=e_codes[:].bitcast(FP8X4),
+                lhsT_scale=e_scales[:],
+                rhs=v_codes[:, h, :].bitcast(FP8X4),
+                rhs_scale=v_scales[:, h, :],
+                start=True,
+                stop=True,
+            )
+            o_sb = work.tile([P, DIM], F32, name="o_sb")
+            nc.scalar.activation(out=o_sb[:], in_=bank[:], func=ACT.Copy, scale=inv_sum[:, n : n + 1])
+            nc.sync.dma_start(out=out_rows[:, a, h * DIM : (h + 1) * DIM], in_=o_sb[:])
+
+        def new_flipped():
+            kT = flipped.tile([P, 2, SEQ, 2], BF16, name="kT")
+            qT = flipped.tile([P, 2, SEQ, 2], BF16, name="qT")
+            return kT, qT
+
+        def flip_quarter(h, part, kT, qT):
+            if part < 2:
+                flip_features(k_sb[h], kT, part)
+            else:
+                flip_features(q_sb[h], qT, part - 2)
+
+        for h in range(HEADS):
+            spread_bias(h)
+        quantise_value()
+        for part in range(4):
+            project_values(0, part)
+            if part > 0:
+                quantise_values(0, part - 1)
+        quantise_values(0, 3)
+        kT, qT = new_flipped()
+        for part in range(4):
+            flip_quarter(0, part, kT, qT)
+
+        e_of = {}
+        grouped_of = {}
+        codes_of = {}
+        for n in range(STEPS + 2):
+            h, part = divmod(n, TILES)
+            prepare = h + 1 < HEADS
+            if n < STEPS:
+                masked = scores(n, qT, kT)
+            if prepare:
+                if part == 0:
+                    next_kT, next_qT = new_flipped()
+                flip_quarter(h + 1, part, next_kT, next_qT)
+            if 1 <= n <= STEPS:
+                grouped_of[n - 1] = flip_weights(e_of[n - 1])
+            if n < STEPS:
+                e_of[n] = exponentials(n, masked)
+            if prepare:
+                project_values(h + 1, part)
+            if 1 <= n <= STEPS:
+                codes_of[n - 1] = quantise_weights(n - 1, grouped_of[n - 1])
+            if prepare:
+                quantise_values(h + 1, part)
+                if part == TILES - 1:
+                    kT, qT = next_kT, next_qT
+            if n >= 2:
+                weighted_values(n - 2, codes_of[n - 2][0], codes_of[n - 2][1])

@@ -23,6 +23,12 @@ TILES = SEQ // P
 STEPS = HEADS * TILES
 SCALE = 1.0 / math.sqrt(DIM)
 
+EXP_LAG = 1
+FLIP_LAG = 2
+CODES_LAG = 3
+OUT_LAG = 4
+V_AHEAD = 2
+
 FLOPS = 3 * HEADS * 2 * SEQ * DIM * DIM
 
 
@@ -32,10 +38,8 @@ def tile_maskedmultiheadattention_pa_e_kernel(tc, q, k, value, mask, Wv_words, W
         ctx.enter_context(tc.manual_schedule())
         keep = ctx.enter_context(tc.tile_pool(name="keep", bufs=1))
         flipped = ctx.enter_context(tc.tile_pool(name="flipped", bufs=2))
-        work = ctx.enter_context(tc.tile_pool(name="work", bufs=3))
-        score_banks = ctx.enter_context(tc.psum_pool(name="score_banks", bufs=3))
-        flip_banks = ctx.enter_context(tc.psum_pool(name="flip_banks", bufs=2))
-        mx_banks = ctx.enter_context(tc.psum_pool(name="mx_banks", bufs=3))
+        work = ctx.enter_context(tc.tile_pool(name="work", bufs=4))
+        banks = ctx.enter_context(tc.psum_pool(name="banks", bufs=8))
 
         ident = keep.tile([P, P], F32, name="ident")
         ones = keep.tile([P, P], BF16, name="ones")
@@ -63,7 +67,9 @@ def tile_maskedmultiheadattention_pa_e_kernel(tc, q, k, value, mask, Wv_words, W
         make_identity(nc, ident[:])
 
         nc.scalar.dma_start(out=bias_row[0:1, :], in_=bv.rearrange("(o h) n -> o (h n)", o=1))
+        nc.sync.dma_start(out=k_sb[0][:], in_=k[0].rearrange("(a p) d -> p a d", p=P))
         nc.sync.dma_start(out=val_sb[:], in_=value.rearrange("(p t) f -> p t f", t=PACK))
+        nc.sync.dma_start(out=q_sb[0][:], in_=q[0].rearrange("(p a) d -> p a d", a=TILES))
         scale_words = Wv_scales.bitcast(I32)
         for quad in range(4):
             nc.sync.dma_start(
@@ -72,24 +78,24 @@ def tile_maskedmultiheadattention_pa_e_kernel(tc, q, k, value, mask, Wv_words, W
             )
         code_words = Wv_words.rearrange("h p n t -> h p (n t)").bitcast(I32)
         nc.sync.dma_start(out=wv_codes[:, 0, :].bitcast(I32), in_=code_words[0])
-        nc.sync.dma_start(out=k_sb[0][:], in_=k[0].rearrange("(a p) d -> p a d", p=P))
-        nc.sync.dma_start(out=q_sb[0][:], in_=q[0].rearrange("(p a) d -> p a d", a=TILES))
+        nc.sync.dma_start(out=k_sb[1][:], in_=k[1].rearrange("(a p) d -> p a d", p=P))
         nc.sync.dma_start(out=mask_sb[:], in_=mask.rearrange("(p a) j -> p a j", a=TILES))
+        nc.sync.dma_start(out=q_sb[1][:], in_=q[1].rearrange("(p a) d -> p a d", a=TILES))
         nc.sync.dma_start(out=wv_codes[:, 1:HEADS, :].bitcast(I32), in_=code_words[1:HEADS].rearrange("h p w -> p h w"))
-        for h in range(1, HEADS):
+        for h in range(2, HEADS):
             nc.sync.dma_start(out=k_sb[h][:], in_=k[h].rearrange("(a p) d -> p a d", p=P))
             nc.sync.dma_start(out=q_sb[h][:], in_=q[h].rearrange("(p a) d -> p a d", a=TILES))
         out_rows = out.rearrange("(p a) n -> p a n", a=TILES)
 
         def spread_bias(h):
-            spread = mx_banks.tile([P, DIM], F32, name="spread", tag="mx")
+            spread = banks.tile([P, DIM], F32, name="spread", tag="bank")
             nc.tensor.matmul(out=spread[:], lhsT=ones[:], rhs=bias_row[:, h * DIM : (h + 1) * DIM], start=True, stop=True)
-            nc.scalar.copy(out=bias_all[:, h, :], in_=spread[:])
+            nc.vector.tensor_copy(out=bias_all[:, h, :], in_=spread[:])
 
         def quantise_value():
             pairs = val_grouped[:].rearrange("f t j x -> f (t j x)").bitcast(F32).rearrange("f (t j u) -> f t j u", t=PACK, u=2)
             for half in range(2):
-                bank = flip_banks.tile([P, 2, 2, P], F32, name="val_bank", tag="flip")
+                bank = banks.tile([P, 2, 2, P], F32, name="val_bank", tag="bank")
                 for tt in range(2):
                     words = val_sb[:, 2 * half + tt, :].bitcast(F32)
                     for u in range(2):
@@ -103,7 +109,7 @@ def tile_maskedmultiheadattention_pa_e_kernel(tc, q, k, value, mask, Wv_words, W
 
         def project_values(h, part):
             cols = slice(part * P, (part + 1) * P)
-            bank = mx_banks.tile([P, PACK, P], F32, name="v_bank", tag="mx")
+            bank = banks.tile([P, PACK, P], F32, name="v_bank", tag="bank")
             for t in range(PACK):
                 nc.tensor.matmul_mx(
                     out=bank[:, t, :],
@@ -130,21 +136,23 @@ def tile_maskedmultiheadattention_pa_e_kernel(tc, q, k, value, mask, Wv_words, W
             )
 
         def flip_features(rows_sb, cols_sb, chunk):
-            bank = flip_banks.tile([P, SEQ], F32, name="flip_bank", tag="flip")
+            bank = banks.tile([P, SEQ], F32, name="flip_bank", tag="bank")
             for a in range(TILES):
                 nc.tensor.transpose(bank[:, a * P : (a + 1) * P], rows_sb[:, a, :].bitcast(F32)[:, chunk * P : (chunk + 1) * P], ident[:])
             nc.scalar.copy(out=cols_sb[:, chunk, :, :].rearrange("w r e -> w (r e)"), in_=bank[:].bitcast(BF16))
 
         def scores(n, qT, kT):
             a = n % TILES
-            bank = score_banks.tile([P, SEQ], F32, name="s_bank", tag="s")
+            bank = banks.tile([P, SEQ], F32, name="s_bank", tag="bank")
             for i in range(4):
                 chunk, e = divmod(i, 2)
                 nc.tensor.matmul(out=bank[:], lhsT=qT[:, chunk, a * P : (a + 1) * P, e], rhs=kT[:, chunk, :, e], start=(i == 0), stop=(i == 3))
             masked = work.tile([P, SEQ], F32, name="masked")
             nc.vector.scalar_tensor_tensor(out=masked[:], in0=bank[:], scalar=SCALE, in1=mask_sb[:, a, :], op0=ALU.mult, op1=ALU.mult)
-            nc.vector.tensor_reduce(out=neg_max[:, n : n + 1], in_=masked[:], axis=AXIS.X, op=ALU.max, negate=True)
             return masked
+
+        def row_maximum(n, masked):
+            nc.vector.tensor_reduce(out=neg_max[:, n : n + 1], in_=masked[:], axis=AXIS.X, op=ALU.max, negate=True)
 
         def exponentials(n, masked):
             e_sb = work.tile([P, SEQ], BF16, name="e_sb")
@@ -152,7 +160,7 @@ def tile_maskedmultiheadattention_pa_e_kernel(tc, q, k, value, mask, Wv_words, W
             return e_sb
 
         def flip_weights(e_sb):
-            bank = flip_banks.tile([P, 2, P], F32, name="e_bank", tag="flip")
+            bank = banks.tile([P, 2, P], F32, name="e_bank", tag="bank")
             words = e_sb[:].bitcast(F32)
             for u in range(2):
                 nc.tensor.transpose(bank[:, u, :], words[:, u : SEQ // 2 : 2], ident[:])
@@ -170,7 +178,7 @@ def tile_maskedmultiheadattention_pa_e_kernel(tc, q, k, value, mask, Wv_words, W
 
         def weighted_values(n, e_codes, e_scales):
             h, a = divmod(n, TILES)
-            bank = mx_banks.tile([P, DIM], F32, name="o_bank", tag="mx")
+            bank = banks.tile([P, DIM], F32, name="o_bank", tag="bank")
             nc.tensor.matmul_mx(
                 out=bank[:],
                 lhsT=e_codes[:].bitcast(FP8X4),
@@ -195,41 +203,45 @@ def tile_maskedmultiheadattention_pa_e_kernel(tc, q, k, value, mask, Wv_words, W
             else:
                 flip_features(q_sb[h], qT, part - 2)
 
+        def project_quarter(g):
+            if g < STEPS:
+                project_values(g // TILES, g % TILES)
+            if 1 <= g <= STEPS:
+                quantise_values((g - 1) // TILES, (g - 1) % TILES)
+
         for h in range(HEADS):
             spread_bias(h)
-        quantise_value()
-        for part in range(4):
-            project_values(0, part)
-            if part > 0:
-                quantise_values(0, part - 1)
-        quantise_values(0, 3)
         kT, qT = new_flipped()
-        for part in range(4):
-            flip_quarter(0, part, kT, qT)
+        flip_quarter(0, 0, kT, qT)
+        flip_quarter(0, 1, kT, qT)
+        quantise_value()
+        flip_quarter(0, 2, kT, qT)
+        flip_quarter(0, 3, kT, qT)
+        for g in range(V_AHEAD):
+            project_quarter(g)
 
+        masked_of = {}
         e_of = {}
         grouped_of = {}
         codes_of = {}
-        for n in range(STEPS + 2):
+        for n in range(STEPS + OUT_LAG):
             h, part = divmod(n, TILES)
-            prepare = h + 1 < HEADS
-            if n < STEPS:
-                masked = scores(n, qT, kT)
-            if prepare:
+            if h + 1 < HEADS:
                 if part == 0:
                     next_kT, next_qT = new_flipped()
                 flip_quarter(h + 1, part, next_kT, next_qT)
-            if 1 <= n <= STEPS:
-                grouped_of[n - 1] = flip_weights(e_of[n - 1])
             if n < STEPS:
-                e_of[n] = exponentials(n, masked)
-            if prepare:
-                project_values(h + 1, part)
-            if 1 <= n <= STEPS:
-                codes_of[n - 1] = quantise_weights(n - 1, grouped_of[n - 1])
-            if prepare:
-                quantise_values(h + 1, part)
-                if part == TILES - 1:
-                    kT, qT = next_kT, next_qT
-            if n >= 2:
-                weighted_values(n - 2, codes_of[n - 2][0], codes_of[n - 2][1])
+                masked_of[n] = scores(n, qT, kT)
+            if 0 <= n - CODES_LAG < STEPS:
+                codes_of[n - CODES_LAG] = quantise_weights(n - CODES_LAG, grouped_of[n - CODES_LAG])
+            if n < STEPS:
+                row_maximum(n, masked_of[n])
+            if 0 <= n - EXP_LAG < STEPS:
+                e_of[n - EXP_LAG] = exponentials(n - EXP_LAG, masked_of[n - EXP_LAG])
+            project_quarter(n + V_AHEAD)
+            if 0 <= n - OUT_LAG < STEPS:
+                weighted_values(n - OUT_LAG, codes_of[n - OUT_LAG][0], codes_of[n - OUT_LAG][1])
+            if 0 <= n - FLIP_LAG < STEPS:
+                grouped_of[n - FLIP_LAG] = flip_weights(e_of[n - FLIP_LAG])
+            if h + 1 < HEADS and part == TILES - 1:
+                kT, qT = next_kT, next_qT

@@ -24,10 +24,10 @@ STEPS = HEADS * TILES
 SCALE = 1.0 / math.sqrt(DIM)
 
 EXP_LAG = 1
-FLIP_LAG = 2
-CODES_LAG = 3
-OUT_LAG = 4
-V_AHEAD = 2
+FLIP_LAG = 3
+CODES_LAG = 4
+OUT_LAG = 6
+V_LAG = 1
 
 FLOPS = 3 * HEADS * 2 * SEQ * DIM * DIM
 
@@ -44,7 +44,7 @@ def tile_maskedmultiheadattention_pa_e_kernel(tc, q, k, value, mask, Wv_words, W
         ident = keep.tile([P, P], F32, name="ident")
         ones = keep.tile([P, P], BF16, name="ones")
         bias_row = keep.tile([P, HEADS * DIM], BF16, name="bias_row")
-        bias_all = keep.tile([P, HEADS, DIM], F32, name="bias_all")
+        bias_all = keep.tile([P, HEADS, DIM], BF16, name="bias_all")
         mask_sb = keep.tile([P, TILES, SEQ], BF16, name="mask_sb")
         val_sb = keep.tile([P, PACK, DIM], BF16, name="val_sb")
         val_grouped = keep.tile([P, PACK, P, PACK], BF16, name="val_grouped", align_bytes=64)
@@ -61,15 +61,15 @@ def tile_maskedmultiheadattention_pa_e_kernel(tc, q, k, value, mask, Wv_words, W
         row_sum = keep.tile([P, STEPS], F32, name="row_sum")
         inv_sum = keep.tile([P, STEPS], F32, name="inv_sum")
 
-        nc.vector.memset(wv_scales[:].rearrange("p h n -> p (h n)").bitcast(I32), 0)
         nc.vector.memset(bias_row[:].bitcast(I32), 0)
         nc.vector.memset(ones[:], 1.0)
+        nc.vector.memset(wv_scales[:].rearrange("p h n -> p (h n)").bitcast(I32), 0)
         make_identity(nc, ident[:])
 
         nc.scalar.dma_start(out=bias_row[0:1, :], in_=bv.rearrange("(o h) n -> o (h n)", o=1))
         nc.sync.dma_start(out=k_sb[0][:], in_=k[0].rearrange("(a p) d -> p a d", p=P))
-        nc.sync.dma_start(out=val_sb[:], in_=value.rearrange("(p t) f -> p t f", t=PACK))
         nc.sync.dma_start(out=q_sb[0][:], in_=q[0].rearrange("(p a) d -> p a d", a=TILES))
+        nc.sync.dma_start(out=val_sb[:], in_=value.rearrange("(p t) f -> p t f", t=PACK))
         scale_words = Wv_scales.bitcast(I32)
         for quad in range(4):
             nc.sync.dma_start(
@@ -87,10 +87,12 @@ def tile_maskedmultiheadattention_pa_e_kernel(tc, q, k, value, mask, Wv_words, W
             nc.sync.dma_start(out=q_sb[h][:], in_=q[h].rearrange("(p a) d -> p a d", a=TILES))
         out_rows = out.rearrange("(p a) n -> p a n", a=TILES)
 
-        def spread_bias(h):
-            spread = banks.tile([P, DIM], F32, name="spread", tag="bank")
-            nc.tensor.matmul(out=spread[:], lhsT=ones[:], rhs=bias_row[:, h * DIM : (h + 1) * DIM], start=True, stop=True)
-            nc.vector.tensor_copy(out=bias_all[:, h, :], in_=spread[:])
+        def spread_bias(pair):
+            spread = banks.tile([P, 2, DIM], BF16, name="spread", tag="bank")
+            for i in range(2):
+                h = 2 * pair + i
+                nc.tensor.matmul(out=spread[:, i, :], lhsT=ones[:], rhs=bias_row[:, h * DIM : (h + 1) * DIM], start=True, stop=True)
+            nc.scalar.copy(out=bias_all[:, 2 * pair : 2 * pair + 2, :], in_=spread[:])
 
         def quantise_value():
             pairs = val_grouped[:].rearrange("f t j x -> f (t j x)").bitcast(F32).rearrange("f (t j u) -> f t j u", t=PACK, u=2)
@@ -141,12 +143,19 @@ def tile_maskedmultiheadattention_pa_e_kernel(tc, q, k, value, mask, Wv_words, W
                 nc.tensor.transpose(bank[:, a * P : (a + 1) * P], rows_sb[:, a, :].bitcast(F32)[:, chunk * P : (chunk + 1) * P], ident[:])
             nc.scalar.copy(out=cols_sb[:, chunk, :, :].rearrange("w r e -> w (r e)"), in_=bank[:].bitcast(BF16))
 
-        def scores(n, qT, kT):
+        def scores_half(n, qT, kT, bank, chunk):
             a = n % TILES
-            bank = banks.tile([P, SEQ], F32, name="s_bank", tag="bank")
-            for i in range(4):
-                chunk, e = divmod(i, 2)
-                nc.tensor.matmul(out=bank[:], lhsT=qT[:, chunk, a * P : (a + 1) * P, e], rhs=kT[:, chunk, :, e], start=(i == 0), stop=(i == 3))
+            for e in range(2):
+                nc.tensor.matmul(
+                    out=bank[:],
+                    lhsT=qT[:, chunk, a * P : (a + 1) * P, e],
+                    rhs=kT[:, chunk, :, e],
+                    start=(chunk == 0 and e == 0),
+                    stop=(chunk == 1 and e == 1),
+                )
+
+        def mask_scores(n, bank):
+            a = n % TILES
             masked = work.tile([P, SEQ], F32, name="masked")
             nc.vector.scalar_tensor_tensor(out=masked[:], in0=bank[:], scalar=SCALE, in1=mask_sb[:, a, :], op0=ALU.mult, op1=ALU.mult)
             return masked
@@ -156,14 +165,21 @@ def tile_maskedmultiheadattention_pa_e_kernel(tc, q, k, value, mask, Wv_words, W
 
         def exponentials(n, masked):
             e_sb = work.tile([P, SEQ], BF16, name="e_sb")
-            nc.scalar.activation(out=e_sb[:], in_=masked[:], func=ACT.Exp, bias=neg_max[:, n : n + 1], scale=1.0, accum_out=row_sum[:, n : n + 1])
+            nc.scalar.activation(
+                out=e_sb[:].rearrange("i (u p x) -> i p u x", u=2, x=2),
+                in_=masked[:].rearrange("i (p u x) -> i p u x", u=2, x=2),
+                func=ACT.Exp,
+                bias=neg_max[:, n : n + 1],
+                scale=1.0,
+                accum_out=row_sum[:, n : n + 1],
+            )
             return e_sb
 
         def flip_weights(e_sb):
             bank = banks.tile([P, 2, P], F32, name="e_bank", tag="bank")
             words = e_sb[:].bitcast(F32)
             for u in range(2):
-                nc.tensor.transpose(bank[:, u, :], words[:, u : SEQ // 2 : 2], ident[:])
+                nc.tensor.transpose(bank[:, u, :], words[:, u * P : (u + 1) * P], ident[:])
             e_grouped = work.tile([P, P, PACK], BF16, name="e_grouped", align_bytes=64)
             pairs = e_grouped[:].rearrange("j i x -> j (i x)").bitcast(F32).rearrange("j (i u) -> j i u", u=2)
             nc.scalar.copy(out=pairs, in_=bank[:].rearrange("j u i -> j i u"))
@@ -203,22 +219,11 @@ def tile_maskedmultiheadattention_pa_e_kernel(tc, q, k, value, mask, Wv_words, W
             else:
                 flip_features(q_sb[h], qT, part - 2)
 
-        def project_quarter(g):
-            if g < STEPS:
-                project_values(g // TILES, g % TILES)
-            if 1 <= g <= STEPS:
-                quantise_values((g - 1) // TILES, (g - 1) % TILES)
-
-        for h in range(HEADS):
-            spread_bias(h)
         kT, qT = new_flipped()
-        flip_quarter(0, 0, kT, qT)
-        flip_quarter(0, 1, kT, qT)
-        quantise_value()
-        flip_quarter(0, 2, kT, qT)
-        flip_quarter(0, 3, kT, qT)
-        for g in range(V_AHEAD):
-            project_quarter(g)
+        for part in range(4):
+            flip_quarter(0, part, kT, qT)
+        for pair in range(HEADS // 2):
+            spread_bias(pair)
 
         masked_of = {}
         e_of = {}
@@ -226,22 +231,32 @@ def tile_maskedmultiheadattention_pa_e_kernel(tc, q, k, value, mask, Wv_words, W
         codes_of = {}
         for n in range(STEPS + OUT_LAG):
             h, part = divmod(n, TILES)
+            g = n - V_LAG
+            if n < STEPS:
+                s_bank = banks.tile([P, SEQ], F32, name="s_bank", tag="bank")
+                scores_half(n, qT, kT, s_bank, 0)
             if h + 1 < HEADS:
                 if part == 0:
                     next_kT, next_qT = new_flipped()
                 flip_quarter(h + 1, part, next_kT, next_qT)
+            if n == 0:
+                quantise_value()
+            if 0 <= n - FLIP_LAG < STEPS:
+                grouped_of[n - FLIP_LAG] = flip_weights(e_of[n - FLIP_LAG])
             if n < STEPS:
-                masked_of[n] = scores(n, qT, kT)
-            if 0 <= n - CODES_LAG < STEPS:
-                codes_of[n - CODES_LAG] = quantise_weights(n - CODES_LAG, grouped_of[n - CODES_LAG])
+                scores_half(n, qT, kT, s_bank, 1)
+                masked_of[n] = mask_scores(n, s_bank)
+            if 0 <= g < STEPS:
+                project_values(g // TILES, g % TILES)
             if n < STEPS:
                 row_maximum(n, masked_of[n])
             if 0 <= n - EXP_LAG < STEPS:
                 e_of[n - EXP_LAG] = exponentials(n - EXP_LAG, masked_of[n - EXP_LAG])
-            project_quarter(n + V_AHEAD)
+            if 0 <= n - CODES_LAG < STEPS:
+                codes_of[n - CODES_LAG] = quantise_weights(n - CODES_LAG, grouped_of[n - CODES_LAG])
+            if 0 <= g < STEPS:
+                quantise_values(g // TILES, g % TILES)
             if 0 <= n - OUT_LAG < STEPS:
                 weighted_values(n - OUT_LAG, codes_of[n - OUT_LAG][0], codes_of[n - OUT_LAG][1])
-            if 0 <= n - FLIP_LAG < STEPS:
-                grouped_of[n - FLIP_LAG] = flip_weights(e_of[n - FLIP_LAG])
             if h + 1 < HEADS and part == TILES - 1:
                 kT, qT = next_kT, next_qT

@@ -27,7 +27,21 @@ EXP_LAG = 1
 FLIP_LAG = 3
 CODES_LAG = 4
 OUT_LAG = 6
-V_LAG = 1
+VAL_STEP = 1
+V_LAG = 2
+WARM = 5
+LOADS = "k0 q0a ma q0b val sc w0 mb k1 q1 w1 k2 q2 k3 q3"
+BIAS_STEP = 1
+BIAS2 = 5
+MID = 1
+HEAD1 = [2, 3, 3, 4]
+REST = [1, 2, 3, 4]
+DOUBLE = 2
+KP = 1
+TAILV = 1
+FL0 = 1
+VOUT = 6
+VALV = 0
 
 FLOPS = 3 * HEADS * 2 * SEQ * DIM * DIM
 
@@ -38,11 +52,12 @@ def tile_maskedmultiheadattention_pa_e_kernel(tc, q, k, value, mask, Wv_words, W
         ctx.enter_context(tc.manual_schedule())
         keep = ctx.enter_context(tc.tile_pool(name="keep", bufs=1))
         flipped = ctx.enter_context(tc.tile_pool(name="flipped", bufs=2))
-        work = ctx.enter_context(tc.tile_pool(name="work", bufs=4))
+        work = ctx.enter_context(tc.tile_pool(name="work", bufs=6))
         banks = ctx.enter_context(tc.psum_pool(name="banks", bufs=8))
 
         ident = keep.tile([P, P], F32, name="ident")
         ones = keep.tile([P, P], BF16, name="ones")
+        warm = keep.tile([P, DIM], BF16, name="warm")
         bias_row = keep.tile([P, HEADS * DIM], BF16, name="bias_row")
         bias_all = keep.tile([P, HEADS, DIM], BF16, name="bias_all")
         mask_sb = keep.tile([P, TILES, SEQ], BF16, name="mask_sb")
@@ -61,30 +76,50 @@ def tile_maskedmultiheadattention_pa_e_kernel(tc, q, k, value, mask, Wv_words, W
         row_sum = keep.tile([P, STEPS], F32, name="row_sum")
         inv_sum = keep.tile([P, STEPS], F32, name="inv_sum")
 
-        nc.vector.memset(bias_row[:].bitcast(I32), 0)
         nc.vector.memset(ones[:], 1.0)
+        nc.vector.memset(warm[:].bitcast(I32), 0)
+        nc.vector.memset(bias_row[:].bitcast(I32), 0)
         nc.vector.memset(wv_scales[:].rearrange("p h n -> p (h n)").bitcast(I32), 0)
         make_identity(nc, ident[:])
 
-        nc.scalar.dma_start(out=bias_row[0:1, :], in_=bv.rearrange("(o h) n -> o (h n)", o=1))
-        nc.sync.dma_start(out=k_sb[0][:], in_=k[0].rearrange("(a p) d -> p a d", p=P))
-        nc.sync.dma_start(out=q_sb[0][:], in_=q[0].rearrange("(p a) d -> p a d", a=TILES))
-        nc.sync.dma_start(out=val_sb[:], in_=value.rearrange("(p t) f -> p t f", t=PACK))
+        nc.gpsimd.dma_start(out=bias_row[0:1, :], in_=bv.rearrange("(o h) n -> o (h n)", o=1))
+        k_rows = k.rearrange("h (a p) d -> h p a d", p=P)
+        q_rows = q.rearrange("h (p a) d -> h p a d", a=TILES)
+        mask_rows = mask.rearrange("(p a) j -> p a j", a=TILES)
         scale_words = Wv_scales.bitcast(I32)
-        for quad in range(4):
-            nc.sync.dma_start(
-                out=wv_scales[32 * quad : 32 * quad + 4, :, :].bitcast(I32),
-                in_=scale_words[:, 4 * quad : 4 * quad + 4, :].rearrange("h r n -> r h n"),
-            )
         code_words = Wv_words.rearrange("h p n t -> h p (n t)").bitcast(I32)
-        nc.sync.dma_start(out=wv_codes[:, 0, :].bitcast(I32), in_=code_words[0])
-        nc.sync.dma_start(out=k_sb[1][:], in_=k[1].rearrange("(a p) d -> p a d", p=P))
-        nc.sync.dma_start(out=mask_sb[:], in_=mask.rearrange("(p a) j -> p a j", a=TILES))
-        nc.sync.dma_start(out=q_sb[1][:], in_=q[1].rearrange("(p a) d -> p a d", a=TILES))
-        nc.sync.dma_start(out=wv_codes[:, 1:HEADS, :].bitcast(I32), in_=code_words[1:HEADS].rearrange("h p w -> p h w"))
-        for h in range(2, HEADS):
-            nc.sync.dma_start(out=k_sb[h][:], in_=k[h].rearrange("(a p) d -> p a d", p=P))
-            nc.sync.dma_start(out=q_sb[h][:], in_=q[h].rearrange("(p a) d -> p a d", a=TILES))
+        first = slice(0, 1)
+        rest = slice(1, TILES)
+        def load(what):
+            if what == "k0":
+                for a in range(0, TILES, KP):
+                    nc.sync.dma_start(out=k_sb[0][:, a:a+KP, :], in_=k_rows[0][:, a:a+KP, :])
+            elif what == "q0a":
+                nc.sync.dma_start(out=q_sb[0][:, first, :], in_=q_rows[0][:, first, :])
+            elif what == "q0b":
+                nc.sync.dma_start(out=q_sb[0][:, rest, :], in_=q_rows[0][:, rest, :])
+            elif what == "ma":
+                nc.sync.dma_start(out=mask_sb[:, first, :], in_=mask_rows[:, first, :])
+            elif what == "mb":
+                nc.sync.dma_start(out=mask_sb[:, rest, :], in_=mask_rows[:, rest, :])
+            elif what == "val":
+                nc.sync.dma_start(out=val_sb[:], in_=value.rearrange("(p t) f -> p t f", t=PACK))
+            elif what == "sc":
+                for quad in range(4):
+                    nc.sync.dma_start(
+                        out=wv_scales[32 * quad : 32 * quad + 4, :, :].bitcast(I32),
+                        in_=scale_words[:, 4 * quad : 4 * quad + 4, :].rearrange("h r n -> r h n"),
+                    )
+            elif what == "w0":
+                nc.sync.dma_start(out=wv_codes[:, 0, :].bitcast(I32), in_=code_words[0])
+            elif what == "w1":
+                nc.sync.dma_start(out=wv_codes[:, 1:HEADS, :].bitcast(I32), in_=code_words[1:HEADS].rearrange("h p w -> p h w"))
+            elif what[0] == "k":
+                nc.sync.dma_start(out=k_sb[int(what[1])][:], in_=k_rows[int(what[1])])
+            else:
+                nc.sync.dma_start(out=q_sb[int(what[1])][:], in_=q_rows[int(what[1])])
+        for what in LOADS.split():
+            load(what)
         out_rows = out.rearrange("(p a) n -> p a n", a=TILES)
 
         def spread_bias(pair):
@@ -102,7 +137,7 @@ def tile_maskedmultiheadattention_pa_e_kernel(tc, q, k, value, mask, Wv_words, W
                     words = val_sb[:, 2 * half + tt, :].bitcast(F32)
                     for u in range(2):
                         nc.tensor.transpose(bank[:, tt, u, :], words[:, u : DIM // 2 : 2], ident[:])
-                nc.vector.tensor_copy(out=pairs[:, 2 * half : 2 * half + 2, :, :], in_=bank[:].rearrange("f tt u j -> f tt j u"))
+                nc.scalar.copy(out=pairs[:, 2 * half : 2 * half + 2, :, :], in_=bank[:].rearrange("f tt u j -> f tt j u"))
             nc.vector.quantize_mx(
                 out=val_codes[:].bitcast(FP8X4),
                 scales=val_scales[:],
@@ -137,11 +172,14 @@ def tile_maskedmultiheadattention_pa_e_kernel(tc, q, k, value, mask, Wv_words, W
                 in_=v_grouped[:, h, cols, :].rearrange("j n t -> j (n t)"),
             )
 
-        def flip_features(rows_sb, cols_sb, chunk):
-            bank = banks.tile([P, SEQ], F32, name="flip_bank", tag="bank")
-            for a in range(TILES):
-                nc.tensor.transpose(bank[:, a * P : (a + 1) * P], rows_sb[:, a, :].bitcast(F32)[:, chunk * P : (chunk + 1) * P], ident[:])
-            nc.scalar.copy(out=cols_sb[:, chunk, :, :].rearrange("w r e -> w (r e)"), in_=bank[:].bitcast(BF16))
+        def flip_features(rows_sb, cols_sb, tiles, copy):
+            width = P * len(tiles)
+            bank = banks.tile([P, 2, width], F32, name="flip_bank%d" % len(tiles), tag="bank")
+            for c in range(2):
+                for i, a in enumerate(tiles):
+                    nc.tensor.transpose(bank[:, c, i * P : (i + 1) * P], rows_sb[:, a, :].bitcast(F32)[:, c * P : (c + 1) * P], ident[:])
+            words = cols_sb[:].rearrange("w c r e -> w (c r e)").bitcast(F32).rearrange("w (c r) -> w c r", c=2)
+            copy(out=words[:, :, tiles[0] * P : tiles[0] * P + width], in_=bank[:])
 
         def scores_half(n, qT, kT, bank, chunk):
             a = n % TILES
@@ -189,8 +227,11 @@ def tile_maskedmultiheadattention_pa_e_kernel(tc, q, k, value, mask, Wv_words, W
             e_codes = work.tile([P, P], U32, name="e_codes", align_bytes=64)
             e_scales = work.tile([P, P], U8, name="e_scales", align_bytes=64)
             nc.vector.quantize_mx(out=e_codes[:].bitcast(FP8X4), scales=e_scales[:], in_=e_grouped[:].rearrange("j i x -> j (i x)"))
-            nc.vector.reciprocal(out=inv_sum[:, n : n + 1], in_=row_sum[:, n : n + 1])
             return e_codes, e_scales
+
+        def invert_sums(h):
+            steps = slice(h * TILES, (h + 1) * TILES)
+            nc.vector.reciprocal(out=inv_sum[:, steps], in_=row_sum[:, steps])
 
         def weighted_values(n, e_codes, e_scales):
             h, a = divmod(n, TILES)
@@ -205,7 +246,10 @@ def tile_maskedmultiheadattention_pa_e_kernel(tc, q, k, value, mask, Wv_words, W
                 stop=True,
             )
             o_sb = work.tile([P, DIM], F32, name="o_sb")
-            nc.scalar.activation(out=o_sb[:], in_=bank[:], func=ACT.Copy, scale=inv_sum[:, n : n + 1])
+            if n >= STEPS - VOUT and n % 2 == 0:
+                nc.vector.tensor_scalar(out=o_sb[:], in0=bank[:], scalar1=inv_sum[:, n : n + 1], scalar2=None, op0=ALU.mult)
+            else:
+                nc.scalar.activation(out=o_sb[:], in_=bank[:], func=ACT.Copy, scale=inv_sum[:, n : n + 1])
             nc.sync.dma_start(out=out_rows[:, a, h * DIM : (h + 1) * DIM], in_=o_sb[:])
 
         def new_flipped():
@@ -213,19 +257,31 @@ def tile_maskedmultiheadattention_pa_e_kernel(tc, q, k, value, mask, Wv_words, W
             qT = flipped.tile([P, 2, SEQ, 2], BF16, name="qT")
             return kT, qT
 
-        def flip_quarter(h, part, kT, qT):
-            if part < 2:
-                flip_features(k_sb[h], kT, part)
-            else:
-                flip_features(q_sb[h], qT, part - 2)
+        def flip_part(h, part, kT, qT):
+            rows_sb, cols_sb = (k_sb[h], kT) if part < 2 else (q_sb[h], qT)
+            flip_features(rows_sb, cols_sb, [2 * (part % 2), 2 * (part % 2) + 1], nc.scalar.copy)
 
+        idle = banks.tile([P, DIM], F32, name="idle", tag="bank")
+        for i in range(WARM):
+            nc.tensor.matmul(out=idle[:], lhsT=ones[:], rhs=warm[:], start=True, stop=True)
         kT, qT = new_flipped()
-        for part in range(4):
-            flip_quarter(0, part, kT, qT)
-        for pair in range(HEADS // 2):
-            spread_bias(pair)
+        for a in range(0, TILES, KP):
+            flip_features(k_sb[0], kT, list(range(a, a + KP)), nc.scalar.copy if (a // KP) % 2 == 0 else nc.vector.tensor_copy)
+        flip_features(q_sb[0], qT, [0], nc.scalar.copy)
 
         masked_of = {}
+        pair_of = {}
+        flips_at = {}
+        for hh in range(1, HEADS):
+            for unit in range(4):
+                flips_at.setdefault((HEAD1 if hh == 1 else [4 * hh - 4 + x for x in REST])[unit], []).append((hh, unit))
+        quarters_at = {}
+        for gg in range(STEPS):
+            if gg < 2 * DOUBLE:
+                st = V_LAG + gg // 2
+            else:
+                st = V_LAG + DOUBLE + (gg - 2 * DOUBLE)
+            quarters_at.setdefault(st, []).append(gg)
         e_of = {}
         grouped_of = {}
         codes_of = {}
@@ -235,28 +291,41 @@ def tile_maskedmultiheadattention_pa_e_kernel(tc, q, k, value, mask, Wv_words, W
             if n < STEPS:
                 s_bank = banks.tile([P, SEQ], F32, name="s_bank", tag="bank")
                 scores_half(n, qT, kT, s_bank, 0)
-            if h + 1 < HEADS:
-                if part == 0:
-                    next_kT, next_qT = new_flipped()
-                flip_quarter(h + 1, part, next_kT, next_qT)
             if n == 0:
+                scores_half(n, qT, kT, s_bank, 1)
+                flip_features(q_sb[0], qT, [1], nc.scalar.copy)
+                flip_features(q_sb[0], qT, [2, 3], nc.vector.tensor_copy)
+            for hh, unit in flips_at.get(n, []):
+                if unit == 0:
+                    pair_of[hh] = new_flipped()
+                flip_part(hh, unit, pair_of[hh][0], pair_of[hh][1])
+            if n == VAL_STEP and MID:
                 quantise_value()
             if 0 <= n - FLIP_LAG < STEPS:
                 grouped_of[n - FLIP_LAG] = flip_weights(e_of[n - FLIP_LAG])
             if n < STEPS:
-                scores_half(n, qT, kT, s_bank, 1)
+                if n > 0:
+                    scores_half(n, qT, kT, s_bank, 1)
                 masked_of[n] = mask_scores(n, s_bank)
-            if 0 <= g < STEPS:
-                project_values(g // TILES, g % TILES)
-            if n < STEPS:
-                row_maximum(n, masked_of[n])
+            if n == BIAS_STEP:
+                spread_bias(0)
+            if n == BIAS2:
+                spread_bias(1)
+            if n == VAL_STEP and not MID:
+                quantise_value()
             if 0 <= n - EXP_LAG < STEPS:
                 e_of[n - EXP_LAG] = exponentials(n - EXP_LAG, masked_of[n - EXP_LAG])
             if 0 <= n - CODES_LAG < STEPS:
                 codes_of[n - CODES_LAG] = quantise_weights(n - CODES_LAG, grouped_of[n - CODES_LAG])
-            if 0 <= g < STEPS:
-                quantise_values(g // TILES, g % TILES)
+            for gg in quarters_at.get(n - 1, []):
+                quantise_values(gg // TILES, gg % TILES)
+            if n < STEPS:
+                row_maximum(n, masked_of[n])
+            for gg in quarters_at.get(n, []):
+                project_values(gg // TILES, gg % TILES)
+            if n >= TILES and part == 1 and h <= HEADS:
+                invert_sums(h - 1)
             if 0 <= n - OUT_LAG < STEPS:
                 weighted_values(n - OUT_LAG, codes_of[n - OUT_LAG][0], codes_of[n - OUT_LAG][1])
             if h + 1 < HEADS and part == TILES - 1:
-                kT, qT = next_kT, next_qT
+                kT, qT = pair_of[h + 1]

@@ -29,18 +29,22 @@ CODES_LAG = 4
 OUT_LAG = 6
 VAL_STEP = 1
 V_LAG = 2
-WARM = 5
+WARM = 4
 LOADS = "k0 q0a ma q0b val sc w0 mb k1 q1 w1 k2 q2 k3 q3"
 BIAS_STEP = 1
-BIAS2 = 5
+GAP = 1
 MID = 1
 HEAD1 = [2, 3, 3, 4]
 REST = [1, 2, 3, 4]
 DOUBLE = 2
 KP = 1
 TAILV = 1
+TF = [1, 0, 0]
+TC = [2, 1, 1]
+TO = [3, 2, 2, 1, 0, 0]
+RECIP_LAST = 1
 FL0 = 1
-VOUT = 6
+VOUT = 4
 VALV = 0
 
 FLOPS = 3 * HEADS * 2 * SEQ * DIM * DIM
@@ -56,9 +60,8 @@ def tile_maskedmultiheadattention_pa_e_kernel(tc, q, k, value, mask, Wv_words, W
         banks = ctx.enter_context(tc.psum_pool(name="banks", bufs=8))
 
         ident = keep.tile([P, P], F32, name="ident")
-        ones = keep.tile([P, P], BF16, name="ones")
-        warm = keep.tile([P, DIM], BF16, name="warm")
-        bias_row = keep.tile([P, HEADS * DIM], BF16, name="bias_row")
+        warm = keep.tile([P, P], BF16, name="warm")
+        bias_words = keep.tile([P, HEADS * DIM // (2 * P)], F32, name="bias_words")
         bias_all = keep.tile([P, HEADS, DIM], BF16, name="bias_all")
         mask_sb = keep.tile([P, TILES, SEQ], BF16, name="mask_sb")
         val_sb = keep.tile([P, PACK, DIM], BF16, name="val_sb")
@@ -76,13 +79,11 @@ def tile_maskedmultiheadattention_pa_e_kernel(tc, q, k, value, mask, Wv_words, W
         row_sum = keep.tile([P, STEPS], F32, name="row_sum")
         inv_sum = keep.tile([P, STEPS], F32, name="inv_sum")
 
-        nc.vector.memset(ones[:], 1.0)
         nc.vector.memset(warm[:].bitcast(I32), 0)
-        nc.vector.memset(bias_row[:].bitcast(I32), 0)
         nc.vector.memset(wv_scales[:].rearrange("p h n -> p (h n)").bitcast(I32), 0)
         make_identity(nc, ident[:])
 
-        nc.gpsimd.dma_start(out=bias_row[0:1, :], in_=bv.rearrange("(o h) n -> o (h n)", o=1))
+        nc.gpsimd.dma_start(out=bias_words[:], in_=bv.rearrange("h n -> (h n)").bitcast(F32).rearrange("(p c) -> p c", p=P))
         k_rows = k.rearrange("h (a p) d -> h p a d", p=P)
         q_rows = q.rearrange("h (p a) d -> h p a d", a=TILES)
         mask_rows = mask.rearrange("(p a) j -> p a j", a=TILES)
@@ -122,12 +123,13 @@ def tile_maskedmultiheadattention_pa_e_kernel(tc, q, k, value, mask, Wv_words, W
             load(what)
         out_rows = out.rearrange("(p a) n -> p a n", a=TILES)
 
-        def spread_bias(pair):
-            spread = banks.tile([P, 2, DIM], BF16, name="spread", tag="bank")
-            for i in range(2):
-                h = 2 * pair + i
-                nc.tensor.matmul(out=spread[:, i, :], lhsT=ones[:], rhs=bias_row[:, h * DIM : (h + 1) * DIM], start=True, stop=True)
-            nc.scalar.copy(out=bias_all[:, 2 * pair : 2 * pair + 2, :], in_=spread[:])
+        def spread_bias(half):
+            bank = banks.tile([P, 4, P], F32, name="bias_bank", tag="bank")
+            for i in range(4):
+                c = 4 * half + i
+                nc.tensor.transpose(bank[:, i, :], bias_words[:, c : c + 1].to_broadcast([P, P]), ident[:])
+            words = bias_all[:].rearrange("m h n -> m (h n)").bitcast(F32).rearrange("m (p c) -> m p c", c=8)
+            nc.scalar.copy(out=words[:, :, 4 * half : 4 * half + 4], in_=bank[:].rearrange("m c p -> m p c"))
 
         def quantise_value():
             pairs = val_grouped[:].rearrange("f t j x -> f (t j x)").bitcast(F32).rearrange("f (t j u) -> f t j u", t=PACK, u=2)
@@ -263,14 +265,24 @@ def tile_maskedmultiheadattention_pa_e_kernel(tc, q, k, value, mask, Wv_words, W
 
         idle = banks.tile([P, DIM], F32, name="idle", tag="bank")
         for i in range(WARM):
-            nc.tensor.matmul(out=idle[:], lhsT=ones[:], rhs=warm[:], start=True, stop=True)
+            nc.tensor.matmul(out=idle[:], lhsT=warm[:], rhs=warm[:, 0:1].to_broadcast([P, DIM]), start=True, stop=True)
         kT, qT = new_flipped()
         for a in range(0, TILES, KP):
             flip_features(k_sb[0], kT, list(range(a, a + KP)), nc.scalar.copy if (a // KP) % 2 == 0 else nc.vector.tensor_copy)
         flip_features(q_sb[0], qT, [0], nc.scalar.copy)
+        for i in range(GAP):
+            nc.tensor.matmul(out=idle[:], lhsT=warm[:], rhs=warm[:, 0:1].to_broadcast([P, DIM]), start=True, stop=True)
 
         masked_of = {}
         pair_of = {}
+        flip_at = {}
+        codes_at = {}
+        out_at = {}
+        for i in range(STEPS):
+            left = STEPS - 1 - i
+            flip_at.setdefault(min(i + FLIP_LAG, STEPS + TF[left]) if left < len(TF) else i + FLIP_LAG, []).append(i)
+            codes_at.setdefault(min(i + CODES_LAG, STEPS + TC[left]) if left < len(TC) else i + CODES_LAG, []).append(i)
+            out_at.setdefault(min(i + OUT_LAG, STEPS + TO[left]) if left < len(TO) else i + OUT_LAG, []).append(i)
         flips_at = {}
         for hh in range(1, HEADS):
             for unit in range(4):
@@ -292,8 +304,8 @@ def tile_maskedmultiheadattention_pa_e_kernel(tc, q, k, value, mask, Wv_words, W
                 s_bank = banks.tile([P, SEQ], F32, name="s_bank", tag="bank")
                 scores_half(n, qT, kT, s_bank, 0)
             if n == 0:
-                scores_half(n, qT, kT, s_bank, 1)
                 flip_features(q_sb[0], qT, [1], nc.scalar.copy)
+                scores_half(n, qT, kT, s_bank, 1)
                 flip_features(q_sb[0], qT, [2, 3], nc.vector.tensor_copy)
             for hh, unit in flips_at.get(n, []):
                 if unit == 0:
@@ -301,31 +313,30 @@ def tile_maskedmultiheadattention_pa_e_kernel(tc, q, k, value, mask, Wv_words, W
                 flip_part(hh, unit, pair_of[hh][0], pair_of[hh][1])
             if n == VAL_STEP and MID:
                 quantise_value()
-            if 0 <= n - FLIP_LAG < STEPS:
-                grouped_of[n - FLIP_LAG] = flip_weights(e_of[n - FLIP_LAG])
+            for i in flip_at.get(n, []):
+                grouped_of[i] = flip_weights(e_of[i])
             if n < STEPS:
                 if n > 0:
                     scores_half(n, qT, kT, s_bank, 1)
                 masked_of[n] = mask_scores(n, s_bank)
             if n == BIAS_STEP:
                 spread_bias(0)
-            if n == BIAS2:
                 spread_bias(1)
             if n == VAL_STEP and not MID:
                 quantise_value()
             if 0 <= n - EXP_LAG < STEPS:
                 e_of[n - EXP_LAG] = exponentials(n - EXP_LAG, masked_of[n - EXP_LAG])
-            if 0 <= n - CODES_LAG < STEPS:
-                codes_of[n - CODES_LAG] = quantise_weights(n - CODES_LAG, grouped_of[n - CODES_LAG])
+            for i in codes_at.get(n, []):
+                codes_of[i] = quantise_weights(i, grouped_of[i])
             for gg in quarters_at.get(n - 1, []):
                 quantise_values(gg // TILES, gg % TILES)
             if n < STEPS:
                 row_maximum(n, masked_of[n])
             for gg in quarters_at.get(n, []):
                 project_values(gg // TILES, gg % TILES)
-            if n >= TILES and part == 1 and h <= HEADS:
+            if n >= TILES and part == (1 if h < HEADS else RECIP_LAST) and h <= HEADS:
                 invert_sums(h - 1)
-            if 0 <= n - OUT_LAG < STEPS:
-                weighted_values(n - OUT_LAG, codes_of[n - OUT_LAG][0], codes_of[n - OUT_LAG][1])
+            for i in out_at.get(n, []):
+                weighted_values(i, codes_of[i][0], codes_of[i][1])
             if h + 1 < HEADS and part == TILES - 1:
                 kT, qT = pair_of[h + 1]

@@ -32,6 +32,7 @@ V_LAG = 2
 WARM = 4
 LOADS = "k0 q0a ma q0b val sc w0 mb k1 q1 w1 k2 q2 k3 q3"
 BIAS_STEP = 1
+WEAVE = [2, 2, 2, 0]
 GAP = 1
 MID = 1
 HEAD1 = [2, 3, 3, 4]
@@ -133,18 +134,26 @@ def tile_maskedmultiheadattention_pa_e_kernel(tc, q, k, value, mask, Wv_words, W
 
         def quantise_value():
             pairs = val_grouped[:].rearrange("f t j x -> f (t j x)").bitcast(F32).rearrange("f (t j u) -> f t j u", t=PACK, u=2)
+            val_banks = []
             for half in range(2):
                 bank = banks.tile([P, 2, 2, P], F32, name="val_bank", tag="bank")
-                for tt in range(2):
-                    words = val_sb[:, 2 * half + tt, :].bitcast(F32)
-                    for u in range(2):
-                        nc.tensor.transpose(bank[:, tt, u, :], words[:, u : DIM // 2 : 2], ident[:])
-                nc.scalar.copy(out=pairs[:, 2 * half : 2 * half + 2, :, :], in_=bank[:].rearrange("f tt u j -> f tt j u"))
-            nc.vector.quantize_mx(
-                out=val_codes[:].bitcast(FP8X4),
-                scales=val_scales[:],
-                in_=val_grouped[:].rearrange("f t j x -> f (t j x)"),
-            )
+                val_banks.append(bank)
+
+            def piece(j):
+                half, tt, u = j // 4, j // 2 % 2, j % 2
+                bank = val_banks[half]
+                words = val_sb[:, 2 * half + tt, :].bitcast(F32)
+                nc.tensor.transpose(bank[:, tt, u, :], words[:, u : DIM // 2 : 2], ident[:])
+                if j % 4 == 3:
+                    nc.scalar.copy(out=pairs[:, 2 * half : 2 * half + 2, :, :], in_=bank[:].rearrange("f tt u j -> f tt j u"))
+                if j == 7:
+                    nc.vector.quantize_mx(
+                        out=val_codes[:].bitcast(FP8X4),
+                        scales=val_scales[:],
+                        in_=val_grouped[:].rearrange("f t j x -> f (t j x)"),
+                    )
+
+            return [(piece, j) for j in range(8)]
 
         def project_values(h, part):
             cols = slice(part * P, (part + 1) * P)
@@ -177,22 +186,26 @@ def tile_maskedmultiheadattention_pa_e_kernel(tc, q, k, value, mask, Wv_words, W
         def flip_features(rows_sb, cols_sb, tiles, copy):
             width = P * len(tiles)
             bank = banks.tile([P, 2, width], F32, name="flip_bank%d" % len(tiles), tag="bank")
-            for c in range(2):
-                for i, a in enumerate(tiles):
-                    nc.tensor.transpose(bank[:, c, i * P : (i + 1) * P], rows_sb[:, a, :].bitcast(F32)[:, c * P : (c + 1) * P], ident[:])
             words = cols_sb[:].rearrange("w c r e -> w (c r e)").bitcast(F32).rearrange("w (c r) -> w c r", c=2)
-            copy(out=words[:, :, tiles[0] * P : tiles[0] * P + width], in_=bank[:])
 
-        def scores_half(n, qT, kT, bank, chunk):
+            def piece(j):
+                c, i = divmod(j, len(tiles))
+                nc.tensor.transpose(bank[:, c, i * P : (i + 1) * P], rows_sb[:, tiles[i], :].bitcast(F32)[:, c * P : (c + 1) * P], ident[:])
+                if j == 2 * len(tiles) - 1:
+                    copy(out=words[:, :, tiles[0] * P : tiles[0] * P + width], in_=bank[:])
+
+            return [(piece, j) for j in range(2 * len(tiles))]
+
+        def scores_part(n, qT, kT, bank, j):
             a = n % TILES
-            for e in range(2):
-                nc.tensor.matmul(
-                    out=bank[:],
-                    lhsT=qT[:, chunk, a * P : (a + 1) * P, e],
-                    rhs=kT[:, chunk, :, e],
-                    start=(chunk == 0 and e == 0),
-                    stop=(chunk == 1 and e == 1),
-                )
+            chunk, e = divmod(j, 2)
+            nc.tensor.matmul(
+                out=bank[:],
+                lhsT=qT[:, chunk, a * P : (a + 1) * P, e],
+                rhs=kT[:, chunk, :, e],
+                start=(j == 0),
+                stop=(j == 3),
+            )
 
         def mask_scores(n, bank):
             a = n % TILES
@@ -218,12 +231,15 @@ def tile_maskedmultiheadattention_pa_e_kernel(tc, q, k, value, mask, Wv_words, W
         def flip_weights(e_sb):
             bank = banks.tile([P, 2, P], F32, name="e_bank", tag="bank")
             words = e_sb[:].bitcast(F32)
-            for u in range(2):
-                nc.tensor.transpose(bank[:, u, :], words[:, u * P : (u + 1) * P], ident[:])
             e_grouped = work.tile([P, P, PACK], BF16, name="e_grouped", align_bytes=64)
             pairs = e_grouped[:].rearrange("j i x -> j (i x)").bitcast(F32).rearrange("j (i u) -> j i u", u=2)
-            nc.scalar.copy(out=pairs, in_=bank[:].rearrange("j u i -> j i u"))
-            return e_grouped
+
+            def piece(u):
+                nc.tensor.transpose(bank[:, u, :], words[:, u * P : (u + 1) * P], ident[:])
+                if u == 1:
+                    nc.scalar.copy(out=pairs, in_=bank[:].rearrange("j u i -> j i u"))
+
+            return e_grouped, [(piece, u) for u in range(2)]
 
         def quantise_weights(n, e_grouped):
             e_codes = work.tile([P, P], U32, name="e_codes", align_bytes=64)
@@ -261,15 +277,19 @@ def tile_maskedmultiheadattention_pa_e_kernel(tc, q, k, value, mask, Wv_words, W
 
         def flip_part(h, part, kT, qT):
             rows_sb, cols_sb = (k_sb[h], kT) if part < 2 else (q_sb[h], qT)
-            flip_features(rows_sb, cols_sb, [2 * (part % 2), 2 * (part % 2) + 1], nc.scalar.copy)
+            return flip_features(rows_sb, cols_sb, [2 * (part % 2), 2 * (part % 2) + 1], nc.scalar.copy)
+
+        def run(pieces):
+            for piece, j in pieces:
+                piece(j)
 
         idle = banks.tile([P, DIM], F32, name="idle", tag="bank")
         for i in range(WARM):
             nc.tensor.matmul(out=idle[:], lhsT=warm[:], rhs=warm[:, 0:1].to_broadcast([P, DIM]), start=True, stop=True)
         kT, qT = new_flipped()
         for a in range(0, TILES, KP):
-            flip_features(k_sb[0], kT, list(range(a, a + KP)), nc.scalar.copy if (a // KP) % 2 == 0 else nc.vector.tensor_copy)
-        flip_features(q_sb[0], qT, [0], nc.scalar.copy)
+            run(flip_features(k_sb[0], kT, list(range(a, a + KP)), nc.scalar.copy if (a // KP) % 2 == 0 else nc.vector.tensor_copy))
+        run(flip_features(q_sb[0], qT, [0], nc.scalar.copy))
         for i in range(GAP):
             nc.tensor.matmul(out=idle[:], lhsT=warm[:], rhs=warm[:, 0:1].to_broadcast([P, DIM]), start=True, stop=True)
 
@@ -300,25 +320,30 @@ def tile_maskedmultiheadattention_pa_e_kernel(tc, q, k, value, mask, Wv_words, W
         for n in range(STEPS + OUT_LAG):
             h, part = divmod(n, TILES)
             g = n - V_LAG
+            pieces = []
             if n < STEPS:
                 s_bank = banks.tile([P, SEQ], F32, name="s_bank", tag="bank")
-                scores_half(n, qT, kT, s_bank, 0)
             if n == 0:
-                flip_features(q_sb[0], qT, [1], nc.scalar.copy)
-                scores_half(n, qT, kT, s_bank, 1)
-                flip_features(q_sb[0], qT, [2, 3], nc.vector.tensor_copy)
+                pieces += flip_features(q_sb[0], qT, [1], nc.scalar.copy)
+                pieces += flip_features(q_sb[0], qT, [2, 3], nc.vector.tensor_copy)
             for hh, unit in flips_at.get(n, []):
                 if unit == 0:
                     pair_of[hh] = new_flipped()
-                flip_part(hh, unit, pair_of[hh][0], pair_of[hh][1])
+                pieces += flip_part(hh, unit, pair_of[hh][0], pair_of[hh][1])
             if n == VAL_STEP and MID:
-                quantise_value()
+                pieces += quantise_value()
             for i in flip_at.get(n, []):
-                grouped_of[i] = flip_weights(e_of[i])
+                grouped_of[i], more = flip_weights(e_of[i])
+                pieces += more
             if n < STEPS:
-                if n > 0:
-                    scores_half(n, qT, kT, s_bank, 1)
+                for j in range(4):
+                    scores_part(n, qT, kT, s_bank, j)
+                    share = WEAVE[j]
+                    run(pieces[:share] if j < 3 else pieces)
+                    pieces = pieces[share:] if j < 3 else []
                 masked_of[n] = mask_scores(n, s_bank)
+            else:
+                run(pieces)
             if n == BIAS_STEP:
                 spread_bias(0)
                 spread_bias(1)

@@ -31,21 +31,27 @@ VAL_STEP = 1
 V_LAG = 2
 WARM = 4
 LOADS = "k0 q0a ma q0b val sc w0 mb k1 q1 w1 k2 q2 k3 q3"
-BIAS_STEP = 1
+BIAS_STEP = 2
+LASTQ = {}
+VSET = [12, 14]
+SPLIT = []
+Q2 = 0
+Q23 = 1
 WEAVE = [2, 2, 2, 0]
+RATE = 1
 GAP = 1
-MID = 1
+MID = 2
 HEAD1 = [2, 3, 3, 4]
 REST = [1, 2, 3, 4]
 DOUBLE = 2
-KP = 1
+KP = 2
 TAILV = 1
 TF = [1, 0, 0]
 TC = [2, 1, 1]
 TO = [3, 2, 2, 1, 0, 0]
 RECIP_LAST = 1
 FL0 = 1
-VOUT = 4
+VOUT = 6
 VALV = 0
 
 FLOPS = 3 * HEADS * 2 * SEQ * DIM * DIM
@@ -57,20 +63,21 @@ def tile_maskedmultiheadattention_pa_e_kernel(tc, q, k, value, mask, Wv_words, W
         ctx.enter_context(tc.manual_schedule())
         keep = ctx.enter_context(tc.tile_pool(name="keep", bufs=1))
         flipped = ctx.enter_context(tc.tile_pool(name="flipped", bufs=2))
-        work = ctx.enter_context(tc.tile_pool(name="work", bufs=6))
+        work = ctx.enter_context(tc.tile_pool(name="work", bufs=10))
         banks = ctx.enter_context(tc.psum_pool(name="banks", bufs=8))
 
         ident = keep.tile([P, P], F32, name="ident")
         warm = keep.tile([P, P], BF16, name="warm")
         bias_words = keep.tile([P, HEADS * DIM // (2 * P)], F32, name="bias_words")
         bias_all = keep.tile([P, HEADS, DIM], BF16, name="bias_all")
+        mask_raw = keep.tile([P, TILES, SEQ], BF16, name="mask_raw")
         mask_sb = keep.tile([P, TILES, SEQ], BF16, name="mask_sb")
         val_sb = keep.tile([P, PACK, DIM], BF16, name="val_sb")
         val_grouped = keep.tile([P, PACK, P, PACK], BF16, name="val_grouped", align_bytes=64)
         val_codes = keep.tile([P, SEQ], U32, name="val_codes", align_bytes=64)
         val_scales = keep.tile([P, SEQ], U8, name="val_scales", align_bytes=64)
         wv_codes = keep.tile([P, HEADS, DIM], U32, name="wv_codes", align_bytes=64)
-        wv_scales = keep.tile([P, HEADS, DIM], U8, name="wv_scales", align_bytes=64)
+        wv_scales = keep.tile([P, DIM], U8, name="wv_scales", align_bytes=64)
         v_grouped = keep.tile([P, HEADS, DIM, PACK], BF16, name="v_grouped", align_bytes=64)
         v_codes = keep.tile([P, HEADS, DIM], U32, name="v_codes", align_bytes=64)
         v_scales = keep.tile([P, HEADS, DIM], U8, name="v_scales", align_bytes=64)
@@ -81,11 +88,11 @@ def tile_maskedmultiheadattention_pa_e_kernel(tc, q, k, value, mask, Wv_words, W
         inv_sum = keep.tile([P, STEPS], F32, name="inv_sum")
 
         nc.vector.memset(warm[:].bitcast(I32), 0)
-        nc.vector.memset(wv_scales[:].rearrange("p h n -> p (h n)").bitcast(I32), 0)
+        nc.vector.memset(wv_scales[:].bitcast(I32), 0)
         make_identity(nc, ident[:])
 
         nc.gpsimd.dma_start(out=bias_words[:], in_=bv.rearrange("h n -> (h n)").bitcast(F32).rearrange("(p c) -> p c", p=P))
-        k_rows = k.rearrange("h (a p) d -> h p a d", p=P)
+        k_rows = k.rearrange("h (p a) d -> h p a d", a=TILES)
         q_rows = q.rearrange("h (p a) d -> h p a d", a=TILES)
         mask_rows = mask.rearrange("(p a) j -> p a j", a=TILES)
         scale_words = Wv_scales.bitcast(I32)
@@ -101,16 +108,16 @@ def tile_maskedmultiheadattention_pa_e_kernel(tc, q, k, value, mask, Wv_words, W
             elif what == "q0b":
                 nc.sync.dma_start(out=q_sb[0][:, rest, :], in_=q_rows[0][:, rest, :])
             elif what == "ma":
-                nc.sync.dma_start(out=mask_sb[:, first, :], in_=mask_rows[:, first, :])
+                nc.sync.dma_start(out=mask_raw[:, first, :], in_=mask_rows[:, first, :])
             elif what == "mb":
-                nc.sync.dma_start(out=mask_sb[:, rest, :], in_=mask_rows[:, rest, :])
+                nc.sync.dma_start(out=mask_raw[:, rest, :], in_=mask_rows[:, rest, :])
             elif what == "val":
                 nc.sync.dma_start(out=val_sb[:], in_=value.rearrange("(p t) f -> p t f", t=PACK))
             elif what == "sc":
                 for quad in range(4):
                     nc.sync.dma_start(
-                        out=wv_scales[32 * quad : 32 * quad + 4, :, :].bitcast(I32),
-                        in_=scale_words[:, 4 * quad : 4 * quad + 4, :].rearrange("h r n -> r h n"),
+                        out=wv_scales[32 * quad : 32 * quad + 16, :].bitcast(I32),
+                        in_=scale_words[:, 4 * quad : 4 * quad + 4, :],
                     )
             elif what == "w0":
                 nc.sync.dma_start(out=wv_codes[:, 0, :].bitcast(I32), in_=code_words[0])
@@ -164,7 +171,7 @@ def tile_maskedmultiheadattention_pa_e_kernel(tc, q, k, value, mask, Wv_words, W
                     lhsT=val_codes[:, t * P : (t + 1) * P].bitcast(FP8X4),
                     lhsT_scale=val_scales[:, t * P : (t + 1) * P],
                     rhs=wv_codes[:, h, cols].bitcast(FP8X4),
-                    rhs_scale=wv_scales[:, h, cols],
+                    rhs_scale=wv_scales[4 * h : P, cols],
                     start=True,
                     stop=True,
                 )
@@ -183,18 +190,51 @@ def tile_maskedmultiheadattention_pa_e_kernel(tc, q, k, value, mask, Wv_words, W
                 in_=v_grouped[:, h, cols, :].rearrange("j n t -> j (n t)"),
             )
 
-        def flip_features(rows_sb, cols_sb, tiles, copy):
+        def flip_keys(h, kT, u):
+            words = kT[:].rearrange("w c r e -> w (c r e)").bitcast(F32).rearrange("w (c r) -> w c r", c=2)
+            bank = banks.tile([P, 2, 2, P], F32, name="key_bank", tag="bank")
+
+            def piece(j):
+                c, x = divmod(j, 2)
+                nc.tensor.transpose(bank[:, c, x, :], k_sb[h][:, 2 * u + x, :].bitcast(F32)[:, c * P : (c + 1) * P], ident[:])
+                if j == 3:
+                    nc.scalar.copy(
+                        out=words[:, :, 2 * P * u : 2 * P * (u + 1)].rearrange("w c (p x) -> w c p x", x=2),
+                        in_=bank[:].rearrange("w c x p -> w c p x"),
+                    )
+
+            return [(piece, j) for j in range(4)]
+
+        def flip_first_keys(kT, u):
+            words = kT[:].rearrange("w c r e -> w (c r e)").bitcast(F32).rearrange("w (c r) -> w c r", c=2)
+            for c in range(2):
+                bank = banks.tile([P, 2, P], F32, name="key_half", tag="bank")
+                for x in range(2):
+                    nc.tensor.transpose(bank[:, x, :], k_sb[0][:, 2 * u + x, :].bitcast(F32)[:, c * P : (c + 1) * P], ident[:])
+                copy = nc.scalar.copy if c == 0 else nc.vector.tensor_copy
+                copy(
+                    out=words[:, c, 2 * P * u : 2 * P * (u + 1)].rearrange("w (p x) -> w p x", x=2),
+                    in_=bank[:].rearrange("w x p -> w p x"),
+                )
+
+        def flip_queries(h, qT, tiles, copy):
             width = P * len(tiles)
-            bank = banks.tile([P, 2, width], F32, name="flip_bank%d" % len(tiles), tag="bank")
-            words = cols_sb[:].rearrange("w c r e -> w (c r e)").bitcast(F32).rearrange("w (c r) -> w c r", c=2)
+            words = qT[:].rearrange("w c r e -> w (c r e)").bitcast(F32).rearrange("w (c r) -> w c r", c=2)
+            bank = banks.tile([P, 2, width], F32, name="query_bank%d" % len(tiles), tag="bank")
 
             def piece(j):
                 c, i = divmod(j, len(tiles))
-                nc.tensor.transpose(bank[:, c, i * P : (i + 1) * P], rows_sb[:, tiles[i], :].bitcast(F32)[:, c * P : (c + 1) * P], ident[:])
+                nc.tensor.transpose(bank[:, c, i * P : (i + 1) * P], q_sb[h][:, tiles[i], :].bitcast(F32)[:, c * P : (c + 1) * P], ident[:])
                 if j == 2 * len(tiles) - 1:
                     copy(out=words[:, :, tiles[0] * P : tiles[0] * P + width], in_=bank[:])
 
             return [(piece, j) for j in range(2 * len(tiles))]
+
+        def sort_mask(tiles):
+            source = mask_raw[:].rearrange("i a j -> i (a j)").bitcast(F32).rearrange("i (a p u) -> i a u p", a=TILES, u=2)
+            target = mask_sb[:].rearrange("i a j -> i (a j)").bitcast(F32).rearrange("i (a u p) -> i a u p", a=TILES, u=2)
+            for a in tiles:
+                nc.vector.tensor_copy(out=target[:, a, :, :], in_=source[:, a, :, :])
 
         def scores_part(n, qT, kT, bank, j):
             a = n % TILES
@@ -219,8 +259,8 @@ def tile_maskedmultiheadattention_pa_e_kernel(tc, q, k, value, mask, Wv_words, W
         def exponentials(n, masked):
             e_sb = work.tile([P, SEQ], BF16, name="e_sb")
             nc.scalar.activation(
-                out=e_sb[:].rearrange("i (u p x) -> i p u x", u=2, x=2),
-                in_=masked[:].rearrange("i (p u x) -> i p u x", u=2, x=2),
+                out=e_sb[:],
+                in_=masked[:],
                 func=ACT.Exp,
                 bias=neg_max[:, n : n + 1],
                 scale=1.0,
@@ -264,11 +304,15 @@ def tile_maskedmultiheadattention_pa_e_kernel(tc, q, k, value, mask, Wv_words, W
                 stop=True,
             )
             o_sb = work.tile([P, DIM], F32, name="o_sb")
-            if n >= STEPS - VOUT and n % 2 == 0:
-                nc.vector.tensor_scalar(out=o_sb[:], in0=bank[:], scalar1=inv_sum[:, n : n + 1], scalar2=None, op0=ALU.mult)
-            else:
-                nc.scalar.activation(out=o_sb[:], in_=bank[:], func=ACT.Copy, scale=inv_sum[:, n : n + 1])
-            nc.sync.dma_start(out=out_rows[:, a, h * DIM : (h + 1) * DIM], in_=o_sb[:])
+            cuts = [0, DIM // 2, DIM] if n in SPLIT else [0, DIM]
+            for i in range(len(cuts) - 1):
+                cols = slice(cuts[i], cuts[i + 1])
+                if n in VSET or i == 1:
+                    nc.vector.tensor_scalar(out=o_sb[:, cols], in0=bank[:, cols], scalar1=inv_sum[:, n : n + 1], scalar2=None, op0=ALU.mult)
+                else:
+                    nc.scalar.activation(out=o_sb[:, cols], in_=bank[:, cols], func=ACT.Copy, scale=inv_sum[:, n : n + 1])
+                queue = nc.scalar if i == 1 and Q2 else nc.sync
+                queue.dma_start(out=out_rows[:, a, h * DIM + cuts[i] : h * DIM + cuts[i + 1]], in_=o_sb[:, cols])
 
         def new_flipped():
             kT = flipped.tile([P, 2, SEQ, 2], BF16, name="kT")
@@ -276,8 +320,9 @@ def tile_maskedmultiheadattention_pa_e_kernel(tc, q, k, value, mask, Wv_words, W
             return kT, qT
 
         def flip_part(h, part, kT, qT):
-            rows_sb, cols_sb = (k_sb[h], kT) if part < 2 else (q_sb[h], qT)
-            return flip_features(rows_sb, cols_sb, [2 * (part % 2), 2 * (part % 2) + 1], nc.scalar.copy)
+            if part < 2:
+                return flip_keys(h, kT, part)
+            return flip_queries(h, qT, [2 * (part - 2), 2 * (part - 2) + 1], nc.scalar.copy)
 
         def run(pieces):
             for piece, j in pieces:
@@ -287,9 +332,10 @@ def tile_maskedmultiheadattention_pa_e_kernel(tc, q, k, value, mask, Wv_words, W
         for i in range(WARM):
             nc.tensor.matmul(out=idle[:], lhsT=warm[:], rhs=warm[:, 0:1].to_broadcast([P, DIM]), start=True, stop=True)
         kT, qT = new_flipped()
-        for a in range(0, TILES, KP):
-            run(flip_features(k_sb[0], kT, list(range(a, a + KP)), nc.scalar.copy if (a // KP) % 2 == 0 else nc.vector.tensor_copy))
-        run(flip_features(q_sb[0], qT, [0], nc.scalar.copy))
+        for u in range(2):
+            flip_first_keys(kT, u)
+        run(flip_queries(0, qT, [0], nc.scalar.copy))
+        sort_mask([0])
         for i in range(GAP):
             nc.tensor.matmul(out=idle[:], lhsT=warm[:], rhs=warm[:, 0:1].to_broadcast([P, DIM]), start=True, stop=True)
 
@@ -312,7 +358,8 @@ def tile_maskedmultiheadattention_pa_e_kernel(tc, q, k, value, mask, Wv_words, W
             if gg < 2 * DOUBLE:
                 st = V_LAG + gg // 2
             else:
-                st = V_LAG + DOUBLE + (gg - 2 * DOUBLE)
+                st = V_LAG + DOUBLE + int((gg - 2 * DOUBLE) * RATE)
+            st = LASTQ.get(gg, st)
             quarters_at.setdefault(st, []).append(gg)
         e_of = {}
         grouped_of = {}
@@ -324,13 +371,13 @@ def tile_maskedmultiheadattention_pa_e_kernel(tc, q, k, value, mask, Wv_words, W
             if n < STEPS:
                 s_bank = banks.tile([P, SEQ], F32, name="s_bank", tag="bank")
             if n == 0:
-                pieces += flip_features(q_sb[0], qT, [1], nc.scalar.copy)
-                pieces += flip_features(q_sb[0], qT, [2, 3], nc.vector.tensor_copy)
+                pieces += flip_queries(0, qT, [1], nc.scalar.copy)
+                pieces += flip_queries(0, qT, [2, 3], nc.scalar.copy if Q23 else nc.vector.tensor_copy)
             for hh, unit in flips_at.get(n, []):
                 if unit == 0:
                     pair_of[hh] = new_flipped()
                 pieces += flip_part(hh, unit, pair_of[hh][0], pair_of[hh][1])
-            if n == VAL_STEP and MID:
+            if n == VAL_STEP and MID == 1:
                 pieces += quantise_value()
             for i in flip_at.get(n, []):
                 grouped_of[i], more = flip_weights(e_of[i])
@@ -344,11 +391,13 @@ def tile_maskedmultiheadattention_pa_e_kernel(tc, q, k, value, mask, Wv_words, W
                 masked_of[n] = mask_scores(n, s_bank)
             else:
                 run(pieces)
+            if n + 1 < TILES:
+                sort_mask([n + 1])
+            if n == VAL_STEP and MID == 2:
+                run(quantise_value())
             if n == BIAS_STEP:
                 spread_bias(0)
                 spread_bias(1)
-            if n == VAL_STEP and not MID:
-                quantise_value()
             if 0 <= n - EXP_LAG < STEPS:
                 e_of[n - EXP_LAG] = exponentials(n - EXP_LAG, masked_of[n - EXP_LAG])
             for i in codes_at.get(n, []):

from contextlib import ExitStack
import math

import concourse.mybir as mybir
from concourse.masks import make_identity

F32 = mybir.dt.float32
BF16 = mybir.dt.bfloat16
I32 = mybir.dt.int32
U32 = mybir.dt.uint32
U8 = mybir.dt.uint8
FP8X4 = mybir.dt.float8_e4m3fn_x4
ALU = mybir.AluOpType
ACT = mybir.ActivationFunctionType
AXIS = mybir.AxisListType

P = 128
PACK = 4
HEADS = 4
SEQ = 512
DIM = 512
TILES = SEQ // P
STEPS = HEADS * TILES
SCALE = 1.0 / math.sqrt(DIM)

EXP_LAG = 1
FLIP_LAG = 3
CODES_LAG = 4
OUT_LAG = 6
VAL_STEP = 1
V_LAG = 2
WARM = 4
LOADS = "k0 q0a ma q0b val sc w0 mb k1 q1 w1 k2 q2 k3 q3"
BIAS_STEP = 2
LASTQ = {}
VSET = [12, 14]
SPLIT = []
Q2 = 0
Q23 = 1
WEAVE = [2, 2, 2, 0]
RATE = 1
GAP = 1
MID = 2
HEAD1 = [2, 3, 3, 4]
REST = [1, 2, 3, 4]
DOUBLE = 2
KP = 2
TAILV = 1
TF = [1, 0, 0]
TC = [2, 1, 1]
TO = [3, 2, 2, 1, 0, 0]
RECIP_LAST = 1
FL0 = 1
VOUT = 6
VALV = 0

FLOPS = 3 * HEADS * 2 * SEQ * DIM * DIM


def tile_maskedmultiheadattention_pa_e_kernel(tc, q, k, value, mask, Wv_words, Wv_scales, bv, out):
    nc = tc.nc
    with ExitStack() as ctx:
        ctx.enter_context(tc.manual_schedule())
        keep = ctx.enter_context(tc.tile_pool(name="keep", bufs=1))
        flipped = ctx.enter_context(tc.tile_pool(name="flipped", bufs=2))
        work = ctx.enter_context(tc.tile_pool(name="work", bufs=10))
        banks = ctx.enter_context(tc.psum_pool(name="banks", bufs=8))

        ident = keep.tile([P, P], F32, name="ident")
        warm = keep.tile([P, P], BF16, name="warm")
        bias_words = keep.tile([P, HEADS * DIM // (2 * P)], F32, name="bias_words")
        bias_all = keep.tile([P, HEADS, DIM], BF16, name="bias_all")
        mask_raw = keep.tile([P, TILES, SEQ], BF16, name="mask_raw")
        mask_sb = keep.tile([P, TILES, SEQ], BF16, name="mask_sb")
        val_sb = keep.tile([P, PACK, DIM], BF16, name="val_sb")
        val_grouped = keep.tile([P, PACK, P, PACK], BF16, name="val_grouped", align_bytes=64)
        val_codes = keep.tile([P, SEQ], U32, name="val_codes", align_bytes=64)
        val_scales = keep.tile([P, SEQ], U8, name="val_scales", align_bytes=64)
        wv_codes = keep.tile([P, HEADS, DIM], U32, name="wv_codes", align_bytes=64)
        wv_scales = keep.tile([P, DIM], U8, name="wv_scales", align_bytes=64)
        v_grouped = keep.tile([P, HEADS, DIM, PACK], BF16, name="v_grouped", align_bytes=64)
        v_codes = keep.tile([P, HEADS, DIM], U32, name="v_codes", align_bytes=64)
        v_scales = keep.tile([P, HEADS, DIM], U8, name="v_scales", align_bytes=64)
        q_sb = [keep.tile([P, TILES, DIM], BF16, name="q_sb%d" % h) for h in range(HEADS)]
        k_sb = [keep.tile([P, TILES, DIM], BF16, name="k_sb%d" % h) for h in range(HEADS)]
        neg_max = keep.tile([P, STEPS], F32, name="neg_max")
        row_sum = keep.tile([P, STEPS], F32, name="row_sum")
        inv_sum = keep.tile([P, STEPS], F32, name="inv_sum")

        nc.vector.memset(warm[:].bitcast(I32), 0)
        nc.vector.memset(wv_scales[:].bitcast(I32), 0)
        make_identity(nc, ident[:])

        nc.gpsimd.dma_start(out=bias_words[:], in_=bv.rearrange("h n -> (h n)").bitcast(F32).rearrange("(p c) -> p c", p=P))
        k_rows = k.rearrange("h (p a) d -> h p a d", a=TILES)
        q_rows = q.rearrange("h (p a) d -> h p a d", a=TILES)
        mask_rows = mask.rearrange("(p a) j -> p a j", a=TILES)
        scale_words = Wv_scales.bitcast(I32)
        code_words = Wv_words.rearrange("h p n t -> h p (n t)").bitcast(I32)
        first = slice(0, 1)
        rest = slice(1, TILES)
        def load(what):
            if what == "k0":
                for a in range(0, TILES, KP):
                    nc.sync.dma_start(out=k_sb[0][:, a:a+KP, :], in_=k_rows[0][:, a:a+KP, :])
            elif what == "q0a":
                nc.sync.dma_start(out=q_sb[0][:, first, :], in_=q_rows[0][:, first, :])
            elif what == "q0b":
                nc.sync.dma_start(out=q_sb[0][:, rest, :], in_=q_rows[0][:, rest, :])
            elif what == "ma":
                nc.sync.dma_start(out=mask_raw[:, first, :], in_=mask_rows[:, first, :])
            elif what == "mb":
                nc.sync.dma_start(out=mask_raw[:, rest, :], in_=mask_rows[:, rest, :])
            elif what == "val":
                nc.sync.dma_start(out=val_sb[:], in_=value.rearrange("(p t) f -> p t f", t=PACK))
            elif what == "sc":
                for quad in range(4):
                    nc.sync.dma_start(
                        out=wv_scales[32 * quad : 32 * quad + 16, :].bitcast(I32),
                        in_=scale_words[:, 4 * quad : 4 * quad + 4, :],
                    )
            elif what == "w0":
                nc.sync.dma_start(out=wv_codes[:, 0, :].bitcast(I32), in_=code_words[0])
            elif what == "w1":
                nc.sync.dma_start(out=wv_codes[:, 1:HEADS, :].bitcast(I32), in_=code_words[1:HEADS].rearrange("h p w -> p h w"))
            elif what[0] == "k":
                nc.sync.dma_start(out=k_sb[int(what[1])][:], in_=k_rows[int(what[1])])
            else:
                nc.sync.dma_start(out=q_sb[int(what[1])][:], in_=q_rows[int(what[1])])
        for what in LOADS.split():
            load(what)
        out_rows = out.rearrange("(p a) n -> p a n", a=TILES)

        def spread_bias(half):
            bank = banks.tile([P, 4, P], F32, name="bias_bank", tag="bank")
            for i in range(4):
                c = 4 * half + i
                nc.tensor.transpose(bank[:, i, :], bias_words[:, c : c + 1].to_broadcast([P, P]), ident[:])
            words = bias_all[:].rearrange("m h n -> m (h n)").bitcast(F32).rearrange("m (p c) -> m p c", c=8)
            nc.scalar.copy(out=words[:, :, 4 * half : 4 * half + 4], in_=bank[:].rearrange("m c p -> m p c"))

        def quantise_value():
            pairs = val_grouped[:].rearrange("f t j x -> f (t j x)").bitcast(F32).rearrange("f (t j u) -> f t j u", t=PACK, u=2)
            val_banks = []
            for half in range(2):
                bank = banks.tile([P, 2, 2, P], F32, name="val_bank", tag="bank")
                val_banks.append(bank)

            def piece(j):
                half, tt, u = j // 4, j // 2 % 2, j % 2
                bank = val_banks[half]
                words = val_sb[:, 2 * half + tt, :].bitcast(F32)
                nc.tensor.transpose(bank[:, tt, u, :], words[:, u : DIM // 2 : 2], ident[:])
                if j % 4 == 3:
                    nc.scalar.copy(out=pairs[:, 2 * half : 2 * half + 2, :, :], in_=bank[:].rearrange("f tt u j -> f tt j u"))
                if j == 7:
                    nc.vector.quantize_mx(
                        out=val_codes[:].bitcast(FP8X4),
                        scales=val_scales[:],
                        in_=val_grouped[:].rearrange("f t j x -> f (t j x)"),
                    )

            return [(piece, j) for j in range(8)]

        def project_values(h, part):
            cols = slice(part * P, (part + 1) * P)
            bank = banks.tile([P, PACK, P], F32, name="v_bank", tag="bank")
            for t in range(PACK):
                nc.tensor.matmul_mx(
                    out=bank[:, t, :],
                    lhsT=val_codes[:, t * P : (t + 1) * P].bitcast(FP8X4),
                    lhsT_scale=val_scales[:, t * P : (t + 1) * P],
                    rhs=wv_codes[:, h, cols].bitcast(FP8X4),
                    rhs_scale=wv_scales[4 * h : P, cols],
                    start=True,
                    stop=True,
                )
            nc.vector.tensor_tensor(
                out=v_grouped[:, h, cols, :],
                in0=bank[:].rearrange("j t n -> j n t"),
                in1=bias_all[:, h, cols].unsqueeze(2).to_broadcast([P, P, PACK]),
                op=ALU.add,
            )

        def quantise_values(h, part):
            cols = slice(part * P, (part + 1) * P)
            nc.vector.quantize_mx(
                out=v_codes[:, h, cols].bitcast(FP8X4),
                scales=v_scales[:, h, cols],
                in_=v_grouped[:, h, cols, :].rearrange("j n t -> j (n t)"),
            )

        def flip_keys(h, kT, u):
            words = kT[:].rearrange("w c r e -> w (c r e)").bitcast(F32).rearrange("w (c r) -> w c r", c=2)
            bank = banks.tile([P, 2, 2, P], F32, name="key_bank", tag="bank")

            def piece(j):
                c, x = divmod(j, 2)
                nc.tensor.transpose(bank[:, c, x, :], k_sb[h][:, 2 * u + x, :].bitcast(F32)[:, c * P : (c + 1) * P], ident[:])
                if j == 3:
                    nc.scalar.copy(
                        out=words[:, :, 2 * P * u : 2 * P * (u + 1)].rearrange("w c (p x) -> w c p x", x=2),
                        in_=bank[:].rearrange("w c x p -> w c p x"),
                    )

            return [(piece, j) for j in range(4)]

        def flip_first_keys(kT, u):
            words = kT[:].rearrange("w c r e -> w (c r e)").bitcast(F32).rearrange("w (c r) -> w c r", c=2)
            for c in range(2):
                bank = banks.tile([P, 2, P], F32, name="key_half", tag="bank")
                for x in range(2):
                    nc.tensor.transpose(bank[:, x, :], k_sb[0][:, 2 * u + x, :].bitcast(F32)[:, c * P : (c + 1) * P], ident[:])
                copy = nc.scalar.copy if c == 0 else nc.vector.tensor_copy
                copy(
                    out=words[:, c, 2 * P * u : 2 * P * (u + 1)].rearrange("w (p x) -> w p x", x=2),
                    in_=bank[:].rearrange("w x p -> w p x"),
                )

        def flip_queries(h, qT, tiles, copy):
            width = P * len(tiles)
            words = qT[:].rearrange("w c r e -> w (c r e)").bitcast(F32).rearrange("w (c r) -> w c r", c=2)
            bank = banks.tile([P, 2, width], F32, name="query_bank%d" % len(tiles), tag="bank")

            def piece(j):
                c, i = divmod(j, len(tiles))
                nc.tensor.transpose(bank[:, c, i * P : (i + 1) * P], q_sb[h][:, tiles[i], :].bitcast(F32)[:, c * P : (c + 1) * P], ident[:])
                if j == 2 * len(tiles) - 1:
                    copy(out=words[:, :, tiles[0] * P : tiles[0] * P + width], in_=bank[:])

            return [(piece, j) for j in range(2 * len(tiles))]

        def sort_mask(tiles):
            source = mask_raw[:].rearrange("i a j -> i (a j)").bitcast(F32).rearrange("i (a p u) -> i a u p", a=TILES, u=2)
            target = mask_sb[:].rearrange("i a j -> i (a j)").bitcast(F32).rearrange("i (a u p) -> i a u p", a=TILES, u=2)
            for a in tiles:
                nc.vector.tensor_copy(out=target[:, a, :, :], in_=source[:, a, :, :])

        def scores_part(n, qT, kT, bank, j):
            a = n % TILES
            chunk, e = divmod(j, 2)
            nc.tensor.matmul(
                out=bank[:],
                lhsT=qT[:, chunk, a * P : (a + 1) * P, e],
                rhs=kT[:, chunk, :, e],
                start=(j == 0),
                stop=(j == 3),
            )

        def mask_scores(n, bank):
            a = n % TILES
            masked = work.tile([P, SEQ], F32, name="masked")
            nc.vector.scalar_tensor_tensor(out=masked[:], in0=bank[:], scalar=SCALE, in1=mask_sb[:, a, :], op0=ALU.mult, op1=ALU.mult)
            return masked

        def row_maximum(n, masked):
            nc.vector.tensor_reduce(out=neg_max[:, n : n + 1], in_=masked[:], axis=AXIS.X, op=ALU.max, negate=True)

        def exponentials(n, masked):
            e_sb = work.tile([P, SEQ], BF16, name="e_sb")
            nc.scalar.activation(
                out=e_sb[:],
                in_=masked[:],
                func=ACT.Exp,
                bias=neg_max[:, n : n + 1],
                scale=1.0,
                accum_out=row_sum[:, n : n + 1],
            )
            return e_sb

        def flip_weights(e_sb):
            bank = banks.tile([P, 2, P], F32, name="e_bank", tag="bank")
            words = e_sb[:].bitcast(F32)
            e_grouped = work.tile([P, P, PACK], BF16, name="e_grouped", align_bytes=64)
            pairs = e_grouped[:].rearrange("j i x -> j (i x)").bitcast(F32).rearrange("j (i u) -> j i u", u=2)

            def piece(u):
                nc.tensor.transpose(bank[:, u, :], words[:, u * P : (u + 1) * P], ident[:])
                if u == 1:
                    nc.scalar.copy(out=pairs, in_=bank[:].rearrange("j u i -> j i u"))

            return e_grouped, [(piece, u) for u in range(2)]

        def quantise_weights(n, e_grouped):
            e_codes = work.tile([P, P], U32, name="e_codes", align_bytes=64)
            e_scales = work.tile([P, P], U8, name="e_scales", align_bytes=64)
            nc.vector.quantize_mx(out=e_codes[:].bitcast(FP8X4), scales=e_scales[:], in_=e_grouped[:].rearrange("j i x -> j (i x)"))
            return e_codes, e_scales

        def invert_sums(h):
            steps = slice(h * TILES, (h + 1) * TILES)
            nc.vector.reciprocal(out=inv_sum[:, steps], in_=row_sum[:, steps])

        def weighted_values(n, e_codes, e_scales):
            h, a = divmod(n, TILES)
            bank = banks.tile([P, DIM], F32, name="o_bank", tag="bank")
            nc.tensor.matmul_mx(
                out=bank[:],
                lhsT=e_codes[:].bitcast(FP8X4),
                lhsT_scale=e_scales[:],
                rhs=v_codes[:, h, :].bitcast(FP8X4),
                rhs_scale=v_scales[:, h, :],
                start=True,
                stop=True,
            )
            o_sb = work.tile([P, DIM], F32, name="o_sb")
            cuts = [0, DIM // 2, DIM] if n in SPLIT else [0, DIM]
            for i in range(len(cuts) - 1):
                cols = slice(cuts[i], cuts[i + 1])
                if n in VSET or i == 1:
                    nc.vector.tensor_scalar(out=o_sb[:, cols], in0=bank[:, cols], scalar1=inv_sum[:, n : n + 1], scalar2=None, op0=ALU.mult)
                else:
                    nc.scalar.activation(out=o_sb[:, cols], in_=bank[:, cols], func=ACT.Copy, scale=inv_sum[:, n : n + 1])
                queue = nc.scalar if i == 1 and Q2 else nc.sync
                queue.dma_start(out=out_rows[:, a, h * DIM + cuts[i] : h * DIM + cuts[i + 1]], in_=o_sb[:, cols])

        def new_flipped():
            kT = flipped.tile([P, 2, SEQ, 2], BF16, name="kT")
            qT = flipped.tile([P, 2, SEQ, 2], BF16, name="qT")
            return kT, qT

        def flip_part(h, part, kT, qT):
            if part < 2:
                return flip_keys(h, kT, part)
            return flip_queries(h, qT, [2 * (part - 2), 2 * (part - 2) + 1], nc.scalar.copy)

        def run(pieces):
            for piece, j in pieces:
                piece(j)

        idle = banks.tile([P, DIM], F32, name="idle", tag="bank")
        for i in range(WARM):
            nc.tensor.matmul(out=idle[:], lhsT=warm[:], rhs=warm[:, 0:1].to_broadcast([P, DIM]), start=True, stop=True)
        kT, qT = new_flipped()
        for u in range(2):
            flip_first_keys(kT, u)
        run(flip_queries(0, qT, [0], nc.scalar.copy))
        sort_mask([0])
        for i in range(GAP):
            nc.tensor.matmul(out=idle[:], lhsT=warm[:], rhs=warm[:, 0:1].to_broadcast([P, DIM]), start=True, stop=True)

        masked_of = {}
        pair_of = {}
        flip_at = {}
        codes_at = {}
        out_at = {}
        for i in range(STEPS):
            left = STEPS - 1 - i
            flip_at.setdefault(min(i + FLIP_LAG, STEPS + TF[left]) if left < len(TF) else i + FLIP_LAG, []).append(i)
            codes_at.setdefault(min(i + CODES_LAG, STEPS + TC[left]) if left < len(TC) else i + CODES_LAG, []).append(i)
            out_at.setdefault(min(i + OUT_LAG, STEPS + TO[left]) if left < len(TO) else i + OUT_LAG, []).append(i)
        flips_at = {}
        for hh in range(1, HEADS):
            for unit in range(4):
                flips_at.setdefault((HEAD1 if hh == 1 else [4 * hh - 4 + x for x in REST])[unit], []).append((hh, unit))
        quarters_at = {}
        for gg in range(STEPS):
            if gg < 2 * DOUBLE:
                st = V_LAG + gg // 2
            else:
                st = V_LAG + DOUBLE + int((gg - 2 * DOUBLE) * RATE)
            st = LASTQ.get(gg, st)
            quarters_at.setdefault(st, []).append(gg)
        e_of = {}
        grouped_of = {}
        codes_of = {}
        for n in range(STEPS + OUT_LAG):
            h, part = divmod(n, TILES)
            g = n - V_LAG
            pieces = []
            if n < STEPS:
                s_bank = banks.tile([P, SEQ], F32, name="s_bank", tag="bank")
            if n == 0:
                pieces += flip_queries(0, qT, [1], nc.scalar.copy)
                pieces += flip_queries(0, qT, [2, 3], nc.scalar.copy if Q23 else nc.vector.tensor_copy)
            for hh, unit in flips_at.get(n, []):
                if unit == 0:
                    pair_of[hh] = new_flipped()
                pieces += flip_part(hh, unit, pair_of[hh][0], pair_of[hh][1])
            if n == VAL_STEP and MID == 1:
                pieces += quantise_value()
            for i in flip_at.get(n, []):
                grouped_of[i], more = flip_weights(e_of[i])
                pieces += more
            if n < STEPS:
                for j in range(4):
                    scores_part(n, qT, kT, s_bank, j)
                    share = WEAVE[j]
                    run(pieces[:share] if j < 3 else pieces)
                    pieces = pieces[share:] if j < 3 else []
                masked_of[n] = mask_scores(n, s_bank)
            else:
                run(pieces)
            if n + 1 < TILES:
                sort_mask([n + 1])
            if n == VAL_STEP and MID == 2:
                run(quantise_value())
            if n == BIAS_STEP:
                spread_bias(0)
                spread_bias(1)
            if 0 <= n - EXP_LAG < STEPS:
                e_of[n - EXP_LAG] = exponentials(n - EXP_LAG, masked_of[n - EXP_LAG])
            for i in codes_at.get(n, []):
                codes_of[i] = quantise_weights(i, grouped_of[i])
            for gg in quarters_at.get(n - 1, []):
                quantise_values(gg // TILES, gg % TILES)
            if n < STEPS:
                row_maximum(n, masked_of[n])
            for gg in quarters_at.get(n, []):
                project_values(gg // TILES, gg % TILES)
            if n >= TILES and part == (1 if h < HEADS else RECIP_LAST) and h <= HEADS:
                invert_sums(h - 1)
            for i in out_at.get(n, []):
                weighted_values(i, codes_of[i][0], codes_of[i][1])
            if h + 1 < HEADS and part == TILES - 1:
                kT, qT = pair_of[h + 1]
